import numpy as np
import ml_dtypes


def mxq(x, axis, fmt="e4m3"):
    dtype, down = {"e4m3": (ml_dtypes.float8_e4m3fn, 7), "e5m2": (ml_dtypes.float8_e5m2, 14)}[fmt]
    v = np.moveaxis(np.asarray(x, np.float32).astype(ml_dtypes.bfloat16).astype(np.float64), axis, -1)
    blocks = v.reshape(v.shape[:-1] + (-1, 32))
    amax = np.abs(blocks).max(-1, keepdims=True)
    byte = np.maximum(np.where(amax > 0, np.frexp(amax)[1] - 1 + 127, 0) - down, 1)
    scale = np.exp2(byte - 127.0)
    codes = (blocks / scale).astype(np.float32).astype(dtype).astype(np.float64)
    return np.moveaxis((codes * scale).reshape(v.shape), -1, axis)


WIDE = False


def mx_kscale(k):
    if not WIDE:
        return np.ones(k)
    levels = np.array([10, -10, 5, -5, 0])
    a = np.random.permutation(np.resize(levels, k // 512 * 4)).reshape(k // 512, 4)
    idx = np.arange(k)
    return np.exp2(a[idx // 512, idx % 128 // 32])


BF16 = ml_dtypes.bfloat16


def bf(x):
    return np.asarray(x, np.float32).astype(BF16)


def f64(x):
    return np.asarray(x).astype(np.float64)


B, N, D, GROUP, E1, S1, E2, HID = 4, 2048, 512, 512, 2, 16, 4, 1024
G = N // GROUP
NS = S1 // E2
M = S1 // NS
P2 = E2 * M
R = B * G * M
EPS = 1e-6
LG = 2.0


def l2norm(t):
    return t / np.sqrt(np.sum(t * t, axis=-1, keepdims=True) + EPS)


def setup_inputs():
    s = mx_kscale(D)
    c = np.sqrt(np.mean(1.0 / s**2))
    y = LG / np.sqrt(D) * np.random.standard_normal((B, G, E1, S1, D)) * s * c
    return {"yn": bf(y),
            "means": bf(y.reshape(B, G, E1, M, NS, D).mean(axis=4)),
            "w_slot2": bf(np.random.standard_normal((E1, D, E2 * D)) / s[:, None] / np.tile(s, E2))}


def reference(yn, means, w_slot2):
    mk = f64(means).transpose(2, 0, 1, 3, 4).reshape(E1, R, D)
    se = mxq(mk, 2, "e4m3") @ mxq(f64(w_slot2), 1, "e4m3")
    se = se.reshape(E1, B, G, M, E2, D).transpose(1, 2, 0, 4, 3, 5)
    se2 = (l2norm(se) * np.sqrt(D)).reshape(B, G, E1, P2, D)
    logits = mxq(f64(yn), 4, "e4m3") @ mxq(se2, 4, "e4m3").swapaxes(3, 4)
    a = np.exp(logits - logits.max(axis=3, keepdims=True))
    disp2 = a / a.sum(axis=3, keepdims=True)
    c = np.exp(logits - logits.max(axis=4, keepdims=True))
    comb2 = c / c.sum(axis=4, keepdims=True)
    return disp2, comb2

@@ -1,0 +1,289 @@
+from contextlib import ExitStack
+
+import concourse.mybir as mybir
+from concourse.masks import make_identity
+
+BF16 = mybir.dt.bfloat16
+F32 = mybir.dt.float32
+U32 = mybir.dt.uint32
+U8 = mybir.dt.uint8
+FP8X4 = mybir.dt.float8_e4m3fn_x4
+ACT = mybir.ActivationFunctionType
+ALU = mybir.AluOpType
+AXIS_X = mybir.AxisListType.X
+
+P = 128
+PACK = 4
+D = P * PACK
+E1 = 2
+E2 = 4
+CHUNKS = E2 * E1
+SEG = 4
+TOK = 16
+SLOTS = E2 * SEG
+GROUPS = 32
+PER_TILE = P // TOK
+TILES = GROUPS // PER_TILE
+EPS = 1e-6
+VECTOR_COLS = 352
+
+FLOPS = 2 * GROUPS * SEG * D * E2 * D + 2 * GROUPS * TOK * SLOTS * D
+
+
+def tile_hierarchicalsoftmoe2dblock_pb_s_kernel(tc, yn, means, w_slot2, out_0, out_1):
+    nc = tc.nc
+    with ExitStack() as ctx:
+        keep = ctx.enter_context(tc.tile_pool(name="keep", bufs=1))
+        stage = ctx.enter_context(tc.tile_pool(name="stage", bufs=3))
+        psum = ctx.enter_context(tc.psum_pool(name="psum", bufs=2))
+        means_sb = keep.tile([P, D], BF16)
+        nc.sync.dma_start(out=means_sb[:], in_=means.rearrange("b g k m d -> (b g k m) d"))
+
+        w_raw = {}
+
+        def load_weights(n):
+            e, k = divmod(n, E1)
+            w_raw[n] = keep.tile([P, PACK, D], BF16, name="w_raw_%d" % n)
+            nc.sync.dma_start(
+                out=w_raw[n][:],
+                in_=w_slot2[k].rearrange("(t p) c -> p t c", p=P)[:, :, e * D : (e + 1) * D],
+            )
+
+        for n in range(E1):
+            load_weights(n)
+        yn_sb = keep.tile([P, TILES, D], BF16)
+        nc.sync.dma_start(
+            out=yn_sb[:],
+            in_=yn.rearrange("b g k s d -> (b g k s) d").rearrange("(i q) d -> q i d", q=P),
+        )
+        for n in range(E1, CHUNKS):
+            load_weights(n)
+
+        ident_bf = keep.tile([P, P], BF16)
+        make_identity(nc, ident_bf[:])
+        ident_f32 = keep.tile([P, P], F32)
+        make_identity(nc, ident_f32[:])
+        warm = keep.tile([P, 2], F32)
+        nc.vector.memset(warm[:], 1.0)
+        nc.scalar.activation(out=warm[:, 1:2], in_=warm[:, 0:1], func=ACT.Abs_reciprocal_sqrt)
+
+        def turn(rows, name):
+            turned = psum.tile([P, PACK, P], BF16, name=name, tag="turned")
+            for t in range(PACK):
+                nc.tensor.transpose(turned[:, t, :], rows[:, t * P : (t + 1) * P], ident_bf[:])
+            return turned
+
+        means_grouped = keep.tile([P, E1, P, PACK], BF16, align_bytes=64)
+        nc.vector.memset(means_grouped[:], 0.0)
+        means_turned = turn(means_sb, "means_turned")
+        for kk in range(E1):
+            nc.vector.tensor_copy(
+                out=means_grouped[:, kk].rearrange("p (a k m) t -> p a k m t", k=E1, m=SEG)[:, :, kk],
+                in_=means_turned[:].rearrange("p t (a k m) -> p a k m t", k=E1, m=SEG)[:, :, kk],
+            )
+        means_codes = keep.tile([P, E1, P], U32, align_bytes=64)
+        means_scales = keep.tile([P, E1, P], U8, align_bytes=64)
+        nc.vector.quantize_mx(
+            out=means_codes[:].rearrange("p k r -> p (k r)").bitcast(FP8X4),
+            scales=means_scales[:].rearrange("p k r -> p (k r)"),
+            in_=means_grouped[:].rearrange("p k r t -> p (k r t)"),
+        )
+        own_group = keep.tile([P, PER_TILE], F32)
+        nc.vector.reduce_sum(
+            out=own_group[:], in_=ident_f32[:].rearrange("q (g s) -> q g s", s=TOK), axis=AXIS_X
+        )
+        logits = keep.tile([P, P], F32)
+        nc.vector.memset(logits[:], 0.0)
+
+        yn_grouped = keep.tile([P, TILES * P, PACK], BF16, align_bytes=64)
+        yn_codes = keep.tile([P, TILES * P], U32, align_bytes=64)
+        yn_scales = keep.tile([P, TILES * P], U8, align_bytes=64)
+
+        def prepare_yn():
+            words = yn_grouped[:].rearrange("p r t -> p (r t)").bitcast(F32)
+            for half in range(2):
+                yn_turned = psum.tile([P, 2, 2, P], F32, name="yn_turned_%d" % half, tag="cross")
+                for j in range(2):
+                    for u in range(2):
+                        nc.tensor.transpose(
+                            yn_turned[:, j, u, :],
+                            yn_sb[:, 2 * half + j, :].bitcast(F32)[:, u * P : (u + 1) * P],
+                            ident_f32[:],
+                        )
+                dst = words[:, half * D : (half + 1) * D].rearrange("p (j r u) -> p j r u", j=2, u=2)
+                src = yn_turned[:].rearrange("p j u r -> p j r u")
+                if half == 0:
+                    nc.vector.tensor_copy(out=dst, in_=src)
+                else:
+                    nc.scalar.copy(out=dst, in_=src)
+            nc.vector.quantize_mx(
+                out=yn_codes[:].bitcast(FP8X4),
+                scales=yn_scales[:],
+                in_=yn_grouped[:].rearrange("p r t -> p (r t)"),
+            )
+
+        w_grouped = {}
+        se_ps = {}
+        se2_turned = {}
+        se2_grouped = {}
+        cross_ps = {}
+        sum_sq = keep.tile([P, E2], F32)
+        inv_norm = keep.tile([P, E2], F32)
+
+        def regroup_weights(n):
+            w_grouped[n] = stage.tile([P, D, PACK], BF16, align_bytes=64, name="w_grouped_%d" % n, tag="w_grouped")
+            nc.vector.tensor_copy(
+                out=w_grouped[n][:, :VECTOR_COLS, :].rearrange("p (c i) t -> p c t i", i=4),
+                in_=w_raw[n][:, :, :VECTOR_COLS].rearrange("p t (c i) -> p c t i", i=4),
+            )
+            nc.scalar.copy(
+                out=w_grouped[n][:, VECTOR_COLS:, :].rearrange("p (c i) t -> p c t i", i=4),
+                in_=w_raw[n][:, :, VECTOR_COLS:].rearrange("p t (c i) -> p c t i", i=4),
+            )
+
+        def first_matmul(n):
+            e, k = divmod(n, E1)
+            w_codes = stage.tile([P, D], U32, align_bytes=64)
+            w_scales = stage.tile([P, D], U8, align_bytes=64)
+            nc.vector.quantize_mx(
+                out=w_codes[:].bitcast(FP8X4),
+                scales=w_scales[:],
+                in_=w_grouped[n][:].rearrange("p c t -> p (c t)"),
+            )
+            if k == 0:
+                se_ps[e] = psum.tile([P, D], F32, name="se_ps_%d" % e, tag="se")
+            nc.tensor.matmul_mx(
+                out=se_ps[e][:],
+                lhsT=means_codes[:, k, :].bitcast(FP8X4),
+                lhsT_scale=means_scales[:, k, :],
+                rhs=w_codes[:].bitcast(FP8X4),
+                rhs_scale=w_scales[:],
+                start=(k == 0),
+                stop=(k == E1 - 1),
+            )
+
+        def normalise_and_turn(e):
+            squares = stage.tile([P, D], BF16)
+            nc.scalar.activation(
+                out=squares[:], in_=se_ps[e][:], func=ACT.Square, accum_out=sum_sq[:, e : e + 1]
+            )
+            nc.scalar.activation(
+                out=inv_norm[:, e : e + 1],
+                in_=sum_sq[:, e : e + 1],
+                func=ACT.Abs_reciprocal_sqrt,
+                scale=1.0 / D,
+                bias=EPS / D,
+            )
+            se2_sb = stage.tile([P, D], BF16)
+            nc.scalar.activation(
+                out=se2_sb[:].rearrange("r (u h p) -> r u h p", u=2, h=2),
+                in_=se_ps[e][:].rearrange("r (u p h) -> r u h p", u=2, h=2),
+                func=ACT.Copy,
+                scale=inv_norm[:, e : e + 1],
+            )
+            se2_turned[e] = turn(se2_sb, "se2_turned_%d" % e)
+
+        def regroup_se2(e):
+            se2_grouped[e] = stage.tile([P, P, PACK], BF16, align_bytes=64, name="se2_grouped_%d" % e, tag="se2_grouped")
+            nc.scalar.copy(out=se2_grouped[e][:], in_=se2_turned[e][:].rearrange("p t r -> p r t"))
+
+        def second_matmul(e):
+            se2_codes = stage.tile([P, P], U32, align_bytes=64)
+            se2_scales = stage.tile([P, P], U8, align_bytes=64)
+            nc.vector.quantize_mx(
+                out=se2_codes[:].bitcast(FP8X4),
+                scales=se2_scales[:],
+                in_=se2_grouped[e][:].rearrange("p r t -> p (r t)"),
+            )
+            cross_ps[e] = psum.tile([P, TILES * TILES, PER_TILE * SEG], F32, name="cross_ps_%d" % e, tag="cross")
+            for i in range(TILES):
+                nc.tensor.matmul_mx(
+                    out=cross_ps[e][:, i * TILES : (i + 1) * TILES, :].rearrange("q b c -> q (b c)"),
+                    lhsT=yn_codes[:, i * P : (i + 1) * P].bitcast(FP8X4),
+                    lhsT_scale=yn_scales[:, i * P : (i + 1) * P],
+                    rhs=se2_codes[:].bitcast(FP8X4),
+                    rhs_scale=se2_scales[:],
+                    start=True,
+                    stop=True,
+                )
+
+        def pick_own_group(e):
+            shape = [P, TILES, PER_TILE, SEG]
+            own_only = stage.tile(shape, F32)
+            nc.vector.tensor_tensor(
+                out=own_only[:],
+                in0=cross_ps[e][:, :: TILES + 1, :].rearrange("q i (g m) -> q i g m", m=SEG),
+                in1=own_group[:].unsqueeze(1).unsqueeze(3).to_broadcast(shape),
+                op=ALU.mult,
+            )
+            nc.vector.tensor_reduce(
+                out=logits[:, : TILES * SLOTS].rearrange("q (i e m) -> q i e m", e=E2, m=SEG)[:, :, e, :],
+                in_=own_only[:].rearrange("q i g m -> q i m g"),
+                axis=AXIS_X,
+                op=ALU.add,
+            )
+
+        def round_step(j):
+            for n in (E1 * j, E1 * j + 1):
+                if n < CHUNKS:
+                    regroup_weights(n)
+                if 0 <= n - 1 < CHUNKS:
+                    first_matmul(n - 1)
+            if 0 <= j - 2 < E2:
+                regroup_se2(j - 2)
+            if 0 <= j - 3 < E2:
+                pick_own_group(j - 3)
+            if 0 <= j - 2 < E2:
+                second_matmul(j - 2)
+            if 0 <= j - 1 < E2:
+                normalise_and_turn(j - 1)
+
+        round_step(0)
+        prepare_yn()
+        for j in range(1, E2 + 3):
+            round_step(j)
+        nc.scalar.activation(out=warm[:, 1:2], in_=inv_norm[:, E2 - 1 : E2], func=ACT.Exp, scale=0.0)
+
+        def powers_of_runs(src, runs, name):
+            shape = [P, runs, TOK]
+            view = src.rearrange("q (a x) -> q a x", x=TOK)
+            top = keep.tile([P, runs], F32, name=name + "_top")
+            nc.vector.tensor_reduce(out=top[:], in_=view, axis=AXIS_X, op=ALU.max)
+            powers = keep.tile(shape, F32, name=name + "_powers")
+            nc.vector.tensor_tensor(
+                out=powers[:], in0=view, in1=top[:].unsqueeze(2).to_broadcast(shape), op=ALU.subtract
+            )
+            nc.scalar.activation(out=powers[:], in_=powers[:], func=ACT.Exp)
+            return powers
+
+        def shares_of_runs(powers, runs, name):
+            shape = [P, runs, TOK]
+            total = keep.tile([P, runs], F32, name=name + "_total")
+            nc.vector.tensor_reduce(out=total[:], in_=powers[:], axis=AXIS_X, op=ALU.add)
+            nc.vector.reciprocal(out=total[:], in_=total[:])
+            shares = keep.tile(shape, F32, name=name + "_shares")
+            nc.vector.tensor_tensor(
+                out=shares[:], in0=powers[:], in1=total[:].unsqueeze(2).to_broadcast(shape), op=ALU.mult
+            )
+            return shares
+
+        def store(out, shares):
+            nc.sync.dma_start(
+                out=out.rearrange("b g k s p -> (b g k s) p").rearrange("(i q) p -> q i p", q=P),
+                in_=shares,
+            )
+
+        logits_t_ps = psum.tile([P, P], F32, tag="se")
+        nc.tensor.transpose(logits_t_ps[:], logits[:], ident_f32[:])
+        comb_powers = powers_of_runs(logits[:, : TILES * SLOTS], TILES, "comb")
+        disp_powers = powers_of_runs(logits_t_ps[:], PER_TILE, "disp")
+        disp_t = shares_of_runs(disp_powers, PER_TILE, "disp")
+        disp_ps = psum.tile([P, P], F32, tag="se")
+        nc.tensor.transpose(disp_ps[:], disp_t[:].rearrange("q a x -> q (a x)"), ident_f32[:])
+        comb = shares_of_runs(comb_powers, TILES, "comb")
+        store(out_1, comb[:])
+        disp = keep.tile([P, TILES, SLOTS], F32)
+        nc.scalar.copy(
+            out=disp[:], in_=disp_ps[:, : TILES * SLOTS].rearrange("q (i p) -> q i p", p=SLOTS)
+        )
+        store(out_0, disp[:])

@@ -25,7 +25,7 @@ GROUPS = 32
 PER_TILE = P // TOK
 TILES = GROUPS // PER_TILE
 EPS = 1e-6
-VECTOR_COLS = 352
+VECTOR_COLS = 320
 
 FLOPS = 2 * GROUPS * SEG * D * E2 * D + 2 * GROUPS * TOK * SLOTS * D
 
@@ -35,7 +35,9 @@ def tile_hierarchicalsoftmoe2dblock_pb_s_kernel(tc, yn, means, w_slot2, out_0, o
     with ExitStack() as ctx:
         keep = ctx.enter_context(tc.tile_pool(name="keep", bufs=1))
         stage = ctx.enter_context(tc.tile_pool(name="stage", bufs=3))
-        psum = ctx.enter_context(tc.psum_pool(name="psum", bufs=2))
+        psum = ctx.enter_context(tc.psum_pool(name="psum", bufs=8))
+        ctx.enter_context(tc.manual_schedule())
+
         means_sb = keep.tile([P, D], BF16)
         nc.sync.dma_start(out=means_sb[:], in_=means.rearrange("b g k m d -> (b g k m) d"))
 
@@ -66,43 +68,47 @@ def tile_hierarchicalsoftmoe2dblock_pb_s_kernel(tc, yn, means, w_slot2, out_0, o
         warm = keep.tile([P, 2], F32)
         nc.vector.memset(warm[:], 1.0)
         nc.scalar.activation(out=warm[:, 1:2], in_=warm[:, 0:1], func=ACT.Abs_reciprocal_sqrt)
+        logits = keep.tile([P, 2, P], F32, align_bytes=64)
+        nc.vector.memset(logits[:], 0.0)
+        shares = keep.tile([P, 2, P], F32, align_bytes=64)
+        nc.vector.memset(shares[:], 0.0)
+        means_grouped = keep.tile([P, E1, P, PACK], BF16, align_bytes=64)
+        nc.vector.memset(means_grouped[:], 0.0)
+        own_group = keep.tile([P, PER_TILE], F32)
+        nc.vector.reduce_sum(
+            out=own_group[:], in_=ident_f32[:].rearrange("q (g s) -> q g s", s=TOK), axis=AXIS_X
+        )
 
         def turn(rows, name):
-            turned = psum.tile([P, PACK, P], BF16, name=name, tag="turned")
+            turned = psum.tile([P, PACK, P], BF16, name=name, tag="bank")
             for t in range(PACK):
                 nc.tensor.transpose(turned[:, t, :], rows[:, t * P : (t + 1) * P], ident_bf[:])
             return turned
 
-        means_grouped = keep.tile([P, E1, P, PACK], BF16, align_bytes=64)
-        nc.vector.memset(means_grouped[:], 0.0)
         means_turned = turn(means_sb, "means_turned")
         for kk in range(E1):
-            nc.vector.tensor_copy(
+            nc.scalar.copy(
                 out=means_grouped[:, kk].rearrange("p (a k m) t -> p a k m t", k=E1, m=SEG)[:, :, kk],
                 in_=means_turned[:].rearrange("p t (a k m) -> p a k m t", k=E1, m=SEG)[:, :, kk],
             )
         means_codes = keep.tile([P, E1, P], U32, align_bytes=64)
         means_scales = keep.tile([P, E1, P], U8, align_bytes=64)
-        nc.vector.quantize_mx(
-            out=means_codes[:].rearrange("p k r -> p (k r)").bitcast(FP8X4),
-            scales=means_scales[:].rearrange("p k r -> p (k r)"),
-            in_=means_grouped[:].rearrange("p k r t -> p (k r t)"),
-        )
-        own_group = keep.tile([P, PER_TILE], F32)
-        nc.vector.reduce_sum(
-            out=own_group[:], in_=ident_f32[:].rearrange("q (g s) -> q g s", s=TOK), axis=AXIS_X
-        )
-        logits = keep.tile([P, P], F32)
-        nc.vector.memset(logits[:], 0.0)
+
+        def quantise_means():
+            nc.vector.quantize_mx(
+                out=means_codes[:].rearrange("p k r -> p (k r)").bitcast(FP8X4),
+                scales=means_scales[:].rearrange("p k r -> p (k r)"),
+                in_=means_grouped[:].rearrange("p k r t -> p (k r t)"),
+            )
 
         yn_grouped = keep.tile([P, TILES * P, PACK], BF16, align_bytes=64)
         yn_codes = keep.tile([P, TILES * P], U32, align_bytes=64)
         yn_scales = keep.tile([P, TILES * P], U8, align_bytes=64)
 
-        def prepare_yn():
+        def regroup_yn():
             words = yn_grouped[:].rearrange("p r t -> p (r t)").bitcast(F32)
             for half in range(2):
-                yn_turned = psum.tile([P, 2, 2, P], F32, name="yn_turned_%d" % half, tag="cross")
+                yn_turned = psum.tile([P, 2, 2, P], F32, name="yn_turned_%d" % half, tag="bank")
                 for j in range(2):
                     for u in range(2):
                         nc.tensor.transpose(
@@ -110,12 +116,12 @@ def tile_hierarchicalsoftmoe2dblock_pb_s_kernel(tc, yn, means, w_slot2, out_0, o
                             yn_sb[:, 2 * half + j, :].bitcast(F32)[:, u * P : (u + 1) * P],
                             ident_f32[:],
                         )
-                dst = words[:, half * D : (half + 1) * D].rearrange("p (j r u) -> p j r u", j=2, u=2)
-                src = yn_turned[:].rearrange("p j u r -> p j r u")
-                if half == 0:
-                    nc.vector.tensor_copy(out=dst, in_=src)
-                else:
-                    nc.scalar.copy(out=dst, in_=src)
+                nc.scalar.copy(
+                    out=words[:, half * D : (half + 1) * D].rearrange("p (j r u) -> p j r u", j=2, u=2),
+                    in_=yn_turned[:].rearrange("p j u r -> p j r u"),
+                )
+
+        def quantise_yn():
             nc.vector.quantize_mx(
                 out=yn_codes[:].bitcast(FP8X4),
                 scales=yn_scales[:],
@@ -124,6 +130,7 @@ def tile_hierarchicalsoftmoe2dblock_pb_s_kernel(tc, yn, means, w_slot2, out_0, o
 
         w_grouped = {}
         se_ps = {}
+        se2_sb = {}
         se2_turned = {}
         se2_grouped = {}
         cross_ps = {}
@@ -131,7 +138,9 @@ def tile_hierarchicalsoftmoe2dblock_pb_s_kernel(tc, yn, means, w_slot2, out_0, o
         inv_norm = keep.tile([P, E2], F32)
 
         def regroup_weights(n):
-            w_grouped[n] = stage.tile([P, D, PACK], BF16, align_bytes=64, name="w_grouped_%d" % n, tag="w_grouped")
+            w_grouped[n] = stage.tile(
+                [P, D, PACK], BF16, align_bytes=64, name="w_grouped_%d" % n, tag="w_grouped"
+            )
             nc.vector.tensor_copy(
                 out=w_grouped[n][:, :VECTOR_COLS, :].rearrange("p (c i) t -> p c t i", i=4),
                 in_=w_raw[n][:, :, :VECTOR_COLS].rearrange("p t (c i) -> p c t i", i=4),
@@ -151,7 +160,7 @@ def tile_hierarchicalsoftmoe2dblock_pb_s_kernel(tc, yn, means, w_slot2, out_0, o
                 in_=w_grouped[n][:].rearrange("p c t -> p (c t)"),
             )
             if k == 0:
-                se_ps[e] = psum.tile([P, D], F32, name="se_ps_%d" % e, tag="se")
+                se_ps[e] = psum.tile([P, D], F32, name="se_ps_%d" % e, tag="bank")
             nc.tensor.matmul_mx(
                 out=se_ps[e][:],
                 lhsT=means_codes[:, k, :].bitcast(FP8X4),
@@ -162,7 +171,7 @@ def tile_hierarchicalsoftmoe2dblock_pb_s_kernel(tc, yn, means, w_slot2, out_0, o
                 stop=(k == E1 - 1),
             )
 
-        def normalise_and_turn(e):
+        def normalise(e):
             squares = stage.tile([P, D], BF16)
             nc.scalar.activation(
                 out=squares[:], in_=se_ps[e][:], func=ACT.Square, accum_out=sum_sq[:, e : e + 1]
@@ -174,18 +183,22 @@ def tile_hierarchicalsoftmoe2dblock_pb_s_kernel(tc, yn, means, w_slot2, out_0, o
                 scale=1.0 / D,
                 bias=EPS / D,
             )
-            se2_sb = stage.tile([P, D], BF16)
+            se2_sb[e] = stage.tile([P, D], BF16, name="se2_sb_%d" % e, tag="se2_sb")
             nc.scalar.activation(
-                out=se2_sb[:].rearrange("r (u h p) -> r u h p", u=2, h=2),
+                out=se2_sb[e][:].rearrange("r (u h p) -> r u h p", u=2, h=2),
                 in_=se_ps[e][:].rearrange("r (u p h) -> r u h p", u=2, h=2),
                 func=ACT.Copy,
                 scale=inv_norm[:, e : e + 1],
             )
-            se2_turned[e] = turn(se2_sb, "se2_turned_%d" % e)
+
+        def turn_se2(e):
+            se2_turned[e] = turn(se2_sb[e], "se2_turned_%d" % e)
 
         def regroup_se2(e):
-            se2_grouped[e] = stage.tile([P, P, PACK], BF16, align_bytes=64, name="se2_grouped_%d" % e, tag="se2_grouped")
-            nc.scalar.copy(out=se2_grouped[e][:], in_=se2_turned[e][:].rearrange("p t r -> p r t"))
+            se2_grouped[e] = stage.tile(
+                [P, P, PACK], BF16, align_bytes=64, name="se2_grouped_%d" % e, tag="se2_grouped"
+            )
+            nc.vector.tensor_copy(out=se2_grouped[e][:], in_=se2_turned[e][:].rearrange("p t r -> p r t"))
 
         def second_matmul(e):
             se2_codes = stage.tile([P, P], U32, align_bytes=64)
@@ -195,7 +208,9 @@ def tile_hierarchicalsoftmoe2dblock_pb_s_kernel(tc, yn, means, w_slot2, out_0, o
                 scales=se2_scales[:],
                 in_=se2_grouped[e][:].rearrange("p r t -> p (r t)"),
             )
-            cross_ps[e] = psum.tile([P, TILES * TILES, PER_TILE * SEG], F32, name="cross_ps_%d" % e, tag="cross")
+            cross_ps[e] = psum.tile(
+                [P, TILES * TILES, PER_TILE * SEG], F32, name="cross_ps_%d" % e, tag="bank"
+            )
             for i in range(TILES):
                 nc.tensor.matmul_mx(
                     out=cross_ps[e][:, i * TILES : (i + 1) * TILES, :].rearrange("q b c -> q (b c)"),
@@ -207,83 +222,75 @@ def tile_hierarchicalsoftmoe2dblock_pb_s_kernel(tc, yn, means, w_slot2, out_0, o
                     stop=True,
                 )
 
-        def pick_own_group(e):
+        own_only = keep.tile([P, TILES, E2, PER_TILE, SEG], F32)
+
+        def zero_other_groups(e):
             shape = [P, TILES, PER_TILE, SEG]
-            own_only = stage.tile(shape, F32)
             nc.vector.tensor_tensor(
-                out=own_only[:],
+                out=own_only[:, :, e, :, :],
                 in0=cross_ps[e][:, :: TILES + 1, :].rearrange("q i (g m) -> q i g m", m=SEG),
                 in1=own_group[:].unsqueeze(1).unsqueeze(3).to_broadcast(shape),
                 op=ALU.mult,
             )
-            nc.vector.tensor_reduce(
-                out=logits[:, : TILES * SLOTS].rearrange("q (i e m) -> q i e m", e=E2, m=SEG)[:, :, e, :],
-                in_=own_only[:].rearrange("q i g m -> q i m g"),
-                axis=AXIS_X,
-                op=ALU.add,
-            )
 
-        def round_step(j):
-            for n in (E1 * j, E1 * j + 1):
-                if n < CHUNKS:
-                    regroup_weights(n)
-                if 0 <= n - 1 < CHUNKS:
-                    first_matmul(n - 1)
-            if 0 <= j - 2 < E2:
-                regroup_se2(j - 2)
-            if 0 <= j - 3 < E2:
-                pick_own_group(j - 3)
-            if 0 <= j - 2 < E2:
-                second_matmul(j - 2)
-            if 0 <= j - 1 < E2:
-                normalise_and_turn(j - 1)
+        regroup_weights(0)
+        quantise_means()
+        regroup_weights(1)
+        regroup_yn()
+        first_matmul(0)
+        for n in range(E1, CHUNKS + 1):
+            if n < CHUNKS:
+                regroup_weights(n)
+            first_matmul(n - 1)
+            if n % E1 == 0 and n >= 2 * E1:
+                turn_se2(n // E1 - 2)
+            if n % E1 == 1:
+                normalise(n // E1 - 1)
 
-        round_step(0)
-        prepare_yn()
-        for j in range(1, E2 + 3):
-            round_step(j)
+        quantise_yn()
+        normalise(E2 - 1)
+        turn_se2(E2 - 1)
         nc.scalar.activation(out=warm[:, 1:2], in_=inv_norm[:, E2 - 1 : E2], func=ACT.Exp, scale=0.0)
+        for e in range(E2):
+            regroup_se2(e)
+            second_matmul(e)
+        for e in range(E2):
+            zero_other_groups(e)
+        used = TILES * SLOTS
+        nc.vector.tensor_reduce(
+            out=logits[:, 0, :used].rearrange("q (a m) -> q a m", m=SEG),
+            in_=own_only[:].rearrange("q i e g m -> q (i e) m g"),
+            axis=AXIS_X,
+            op=ALU.add,
+        )
 
-        def powers_of_runs(src, runs, name):
-            shape = [P, runs, TOK]
-            view = src.rearrange("q (a x) -> q a x", x=TOK)
-            top = keep.tile([P, runs], F32, name=name + "_top")
-            nc.vector.tensor_reduce(out=top[:], in_=view, axis=AXIS_X, op=ALU.max)
-            powers = keep.tile(shape, F32, name=name + "_powers")
-            nc.vector.tensor_tensor(
-                out=powers[:], in0=view, in1=top[:].unsqueeze(2).to_broadcast(shape), op=ALU.subtract
-            )
-            nc.scalar.activation(out=powers[:], in_=powers[:], func=ACT.Exp)
-            return powers
+        nc.vector.transpose(out=logits[:, 1, :], in_=logits[:, 0, :])
+        runs = [P, 2, TILES, TOK]
+        top = keep.tile([P, 2, TILES], F32)
+        powers = keep.tile(runs, F32)
+        total = keep.tile([P, 2, TILES], F32)
+        logit_runs = logits[:, :, :used].rearrange("q h (a x) -> q h a x", x=TOK)
+        nc.vector.tensor_reduce(out=top[:], in_=logit_runs, axis=AXIS_X, op=ALU.max)
+        nc.vector.tensor_tensor(
+            out=powers[:], in0=logit_runs, in1=top[:].unsqueeze(3).to_broadcast(runs), op=ALU.subtract
+        )
+        nc.scalar.activation(out=powers[:], in_=powers[:], func=ACT.Exp)
+        nc.vector.tensor_reduce(out=total[:], in_=powers[:], axis=AXIS_X, op=ALU.add)
+        nc.vector.reciprocal(out=total[:], in_=total[:])
+        nc.vector.tensor_tensor(
+            out=shares[:, :, :used].rearrange("q h (a x) -> q h a x", x=TOK),
+            in0=powers[:],
+            in1=total[:].unsqueeze(3).to_broadcast(runs),
+            op=ALU.mult,
+        )
 
-        def shares_of_runs(powers, runs, name):
-            shape = [P, runs, TOK]
-            total = keep.tile([P, runs], F32, name=name + "_total")
-            nc.vector.tensor_reduce(out=total[:], in_=powers[:], axis=AXIS_X, op=ALU.add)
-            nc.vector.reciprocal(out=total[:], in_=total[:])
-            shares = keep.tile(shape, F32, name=name + "_shares")
-            nc.vector.tensor_tensor(
-                out=shares[:], in0=powers[:], in1=total[:].unsqueeze(2).to_broadcast(shape), op=ALU.mult
-            )
-            return shares
-
-        def store(out, shares):
+        def store(out, rows):
             nc.sync.dma_start(
                 out=out.rearrange("b g k s p -> (b g k s) p").rearrange("(i q) p -> q i p", q=P),
-                in_=shares,
+                in_=rows.rearrange("q (i p) -> q i p", p=SLOTS),
             )
 
-        logits_t_ps = psum.tile([P, P], F32, tag="se")
-        nc.tensor.transpose(logits_t_ps[:], logits[:], ident_f32[:])
-        comb_powers = powers_of_runs(logits[:, : TILES * SLOTS], TILES, "comb")
-        disp_powers = powers_of_runs(logits_t_ps[:], PER_TILE, "disp")
-        disp_t = shares_of_runs(disp_powers, PER_TILE, "disp")
-        disp_ps = psum.tile([P, P], F32, tag="se")
-        nc.tensor.transpose(disp_ps[:], disp_t[:].rearrange("q a x -> q (a x)"), ident_f32[:])
-        comb = shares_of_runs(comb_powers, TILES, "comb")
-        store(out_1, comb[:])
-        disp = keep.tile([P, TILES, SLOTS], F32)
-        nc.scalar.copy(
-            out=disp[:], in_=disp_ps[:, : TILES * SLOTS].rearrange("q (i p) -> q i p", p=SLOTS)
-        )
-        store(out_0, disp[:])
+        store(out_1, shares[:, 0, :used])
+        disp = keep.tile([P, P], F32, align_bytes=64)
+        nc.vector.transpose(out=disp[:], in_=shares[:, 1, :])
+        store(out_0, disp[:, :used])

@@ -35,7 +35,8 @@ def tile_hierarchicalsoftmoe2dblock_pb_s_kernel(tc, yn, means, w_slot2, out_0, o
     with ExitStack() as ctx:
         keep = ctx.enter_context(tc.tile_pool(name="keep", bufs=1))
         stage = ctx.enter_context(tc.tile_pool(name="stage", bufs=3))
-        psum = ctx.enter_context(tc.psum_pool(name="psum", bufs=8))
+        psum = ctx.enter_context(tc.psum_pool(name="psum", bufs=6))
+        psum_yn = ctx.enter_context(tc.psum_pool(name="psum_yn", bufs=2))
         ctx.enter_context(tc.manual_schedule())
 
         means_sb = keep.tile([P, D], BF16)
@@ -51,15 +52,13 @@ def tile_hierarchicalsoftmoe2dblock_pb_s_kernel(tc, yn, means, w_slot2, out_0, o
                 in_=w_slot2[k].rearrange("(t p) c -> p t c", p=P)[:, :, e * D : (e + 1) * D],
             )
 
-        for n in range(E1):
+        for n in range(CHUNKS):
             load_weights(n)
         yn_sb = keep.tile([P, TILES, D], BF16)
         nc.sync.dma_start(
             out=yn_sb[:],
             in_=yn.rearrange("b g k s d -> (b g k s) d").rearrange("(i q) d -> q i d", q=P),
         )
-        for n in range(E1, CHUNKS):
-            load_weights(n)
 
         ident_bf = keep.tile([P, P], BF16)
         make_identity(nc, ident_bf[:])
@@ -105,21 +104,25 @@ def tile_hierarchicalsoftmoe2dblock_pb_s_kernel(tc, yn, means, w_slot2, out_0, o
         yn_codes = keep.tile([P, TILES * P], U32, align_bytes=64)
         yn_scales = keep.tile([P, TILES * P], U8, align_bytes=64)
 
-        def regroup_yn():
-            words = yn_grouped[:].rearrange("p r t -> p (r t)").bitcast(F32)
+        yn_turned = {}
+
+        def turn_yn():
             for half in range(2):
-                yn_turned = psum.tile([P, 2, 2, P], F32, name="yn_turned_%d" % half, tag="bank")
+                yn_turned[half] = psum_yn.tile([P, 2, 2, P], F32, name="yn_turned_%d" % half, tag="yn")
                 for j in range(2):
                     for u in range(2):
                         nc.tensor.transpose(
-                            yn_turned[:, j, u, :],
+                            yn_turned[half][:, j, u, :],
                             yn_sb[:, 2 * half + j, :].bitcast(F32)[:, u * P : (u + 1) * P],
                             ident_f32[:],
                         )
-                nc.scalar.copy(
-                    out=words[:, half * D : (half + 1) * D].rearrange("p (j r u) -> p j r u", j=2, u=2),
-                    in_=yn_turned[:].rearrange("p j u r -> p j r u"),
-                )
+
+        def regroup_yn(half):
+            words = yn_grouped[:].rearrange("p r t -> p (r t)").bitcast(F32)
+            nc.scalar.copy(
+                out=words[:, half * D : (half + 1) * D].rearrange("p (j r u) -> p j r u", j=2, u=2),
+                in_=yn_turned[half][:].rearrange("p j u r -> p j r u"),
+            )
 
         def quantise_yn():
             nc.vector.quantize_mx(
@@ -200,14 +203,17 @@ def tile_hierarchicalsoftmoe2dblock_pb_s_kernel(tc, yn, means, w_slot2, out_0, o
             )
             nc.vector.tensor_copy(out=se2_grouped[e][:], in_=se2_turned[e][:].rearrange("p t r -> p r t"))
 
-        def second_matmul(e):
-            se2_codes = stage.tile([P, P], U32, align_bytes=64)
-            se2_scales = stage.tile([P, P], U8, align_bytes=64)
+        se2_codes = keep.tile([P, E2, P], U32, align_bytes=64)
+        se2_scales = keep.tile([P, E2, P], U8, align_bytes=64)
+
+        def quantise_se2(e):
             nc.vector.quantize_mx(
-                out=se2_codes[:].bitcast(FP8X4),
-                scales=se2_scales[:],
+                out=se2_codes[:, e, :].bitcast(FP8X4),
+                scales=se2_scales[:, e, :],
                 in_=se2_grouped[e][:].rearrange("p r t -> p (r t)"),
             )
+
+        def second_matmul(e):
             cross_ps[e] = psum.tile(
                 [P, TILES * TILES, PER_TILE * SEG], F32, name="cross_ps_%d" % e, tag="bank"
             )
@@ -216,8 +222,8 @@ def tile_hierarchicalsoftmoe2dblock_pb_s_kernel(tc, yn, means, w_slot2, out_0, o
                     out=cross_ps[e][:, i * TILES : (i + 1) * TILES, :].rearrange("q b c -> q (b c)"),
                     lhsT=yn_codes[:, i * P : (i + 1) * P].bitcast(FP8X4),
                     lhsT_scale=yn_scales[:, i * P : (i + 1) * P],
-                    rhs=se2_codes[:].bitcast(FP8X4),
-                    rhs_scale=se2_scales[:],
+                    rhs=se2_codes[:, e, :].bitcast(FP8X4),
+                    rhs_scale=se2_scales[:, e, :],
                     start=True,
                     stop=True,
                 )
@@ -233,27 +239,38 @@ def tile_hierarchicalsoftmoe2dblock_pb_s_kernel(tc, yn, means, w_slot2, out_0, o
                 op=ALU.mult,
             )
 
-        regroup_weights(0)
-        quantise_means()
-        regroup_weights(1)
-        regroup_yn()
-        first_matmul(0)
-        for n in range(E1, CHUNKS + 1):
+        def stream_step(n):
             if n < CHUNKS:
                 regroup_weights(n)
             first_matmul(n - 1)
             if n % E1 == 0 and n >= 2 * E1:
                 turn_se2(n // E1 - 2)
-            if n % E1 == 1:
+            if n % E1 == 1 and n >= E1 + 1:
                 normalise(n // E1 - 1)
 
-        quantise_yn()
-        normalise(E2 - 1)
-        turn_se2(E2 - 1)
-        nc.scalar.activation(out=warm[:, 1:2], in_=inv_norm[:, E2 - 1 : E2], func=ACT.Exp, scale=0.0)
-        for e in range(E2):
+        regroup_weights(0)
+        quantise_means()
+        for n in range(1, CHUNKS - 1):
+            stream_step(n)
+        turn_yn()
+        for n in range(CHUNKS - 1, CHUNKS + 1):
+            stream_step(n)
+
+        last = E2 - 1
+        regroup_yn(0)
+        normalise(last)
+        turn_se2(last)
+        regroup_yn(1)
+        nc.scalar.activation(out=warm[:, 1:2], in_=inv_norm[:, last : last + 1], func=ACT.Exp, scale=0.0)
+        for e in range(last):
             regroup_se2(e)
+            quantise_se2(e)
+        quantise_yn()
+        for e in range(last):
             second_matmul(e)
+        regroup_se2(last)
+        quantise_se2(last)
+        second_matmul(last)
         for e in range(E2):
             zero_other_groups(e)
         used = TILES * SLOTS

@@ -119,7 +119,7 @@ def tile_hierarchicalsoftmoe2dblock_pb_s_kernel(tc, yn, means, w_slot2, out_0, o
 
         def regroup_yn(half):
             words = yn_grouped[:].rearrange("p r t -> p (r t)").bitcast(F32)
-            nc.scalar.copy(
+            nc.vector.tensor_copy(
                 out=words[:, half * D : (half + 1) * D].rearrange("p (j r u) -> p j r u", j=2, u=2),
                 in_=yn_turned[half][:].rearrange("p j u r -> p j r u"),
             )
@@ -201,7 +201,7 @@ def tile_hierarchicalsoftmoe2dblock_pb_s_kernel(tc, yn, means, w_slot2, out_0, o
             se2_grouped[e] = stage.tile(
                 [P, P, PACK], BF16, align_bytes=64, name="se2_grouped_%d" % e, tag="se2_grouped"
             )
-            nc.vector.tensor_copy(out=se2_grouped[e][:], in_=se2_turned[e][:].rearrange("p t r -> p r t"))
+            nc.scalar.copy(out=se2_grouped[e][:], in_=se2_turned[e][:].rearrange("p t r -> p r t"))
 
         se2_codes = keep.tile([P, E2, P], U32, align_bytes=64)
         se2_scales = keep.tile([P, E2, P], U8, align_bytes=64)
@@ -239,38 +239,34 @@ def tile_hierarchicalsoftmoe2dblock_pb_s_kernel(tc, yn, means, w_slot2, out_0, o
                 op=ALU.mult,
             )
 
-        def stream_step(n):
-            if n < CHUNKS:
-                regroup_weights(n)
+        regroup_weights(0)
+        quantise_means()
+        for n in range(1, CHUNKS):
+            regroup_weights(n)
             first_matmul(n - 1)
             if n % E1 == 0 and n >= 2 * E1:
                 turn_se2(n // E1 - 2)
             if n % E1 == 1 and n >= E1 + 1:
                 normalise(n // E1 - 1)
 
-        regroup_weights(0)
-        quantise_means()
-        for n in range(1, CHUNKS - 1):
-            stream_step(n)
-        turn_yn()
-        for n in range(CHUNKS - 1, CHUNKS + 1):
-            stream_step(n)
-
         last = E2 - 1
-        regroup_yn(0)
+        first_matmul(CHUNKS - 1)
+        turn_yn()
+        turn_se2(last - 1)
+        regroup_se2(0)
         normalise(last)
         turn_se2(last)
-        regroup_yn(1)
-        nc.scalar.activation(out=warm[:, 1:2], in_=inv_norm[:, last : last + 1], func=ACT.Exp, scale=0.0)
-        for e in range(last):
+        for e in range(1, E2):
             regroup_se2(e)
-            quantise_se2(e)
+        nc.scalar.activation(out=warm[:, 1:2], in_=inv_norm[:, last : last + 1], func=ACT.Exp, scale=0.0)
+        quantise_se2(0)
+        for half in range(2):
+            regroup_yn(half)
         quantise_yn()
-        for e in range(last):
+        for e in range(1, E2):
+            quantise_se2(e)
+        for e in range(E2):
             second_matmul(e)
-        regroup_se2(last)
-        quantise_se2(last)
-        second_matmul(last)
         for e in range(E2):
             zero_other_groups(e)
         used = TILES * SLOTS

@@ -77,6 +77,7 @@ def tile_hierarchicalsoftmoe2dblock_pb_s_kernel(tc, yn, means, w_slot2, out_0, o
         nc.vector.reduce_sum(
             out=own_group[:], in_=ident_f32[:].rearrange("q (g s) -> q g s", s=TOK), axis=AXIS_X
         )
+        nc.vector.tensor_scalar_mul(own_group[:], own_group[:], -1.0)
 
         def turn(rows, name):
             turned = psum.tile([P, PACK, P], BF16, name=name, tag="bank")
@@ -228,15 +229,25 @@ def tile_hierarchicalsoftmoe2dblock_pb_s_kernel(tc, yn, means, w_slot2, out_0, o
                     stop=True,
                 )
 
-        own_only = keep.tile([P, TILES, E2, PER_TILE, SEG], F32)
+        own_only = keep.tile([P, E2, TILES, SEG, PER_TILE], F32)
 
         def zero_other_groups(e):
-            shape = [P, TILES, PER_TILE, SEG]
+            shape = [P, TILES, SEG, PER_TILE]
             nc.vector.tensor_tensor(
-                out=own_only[:, :, e, :, :],
-                in0=cross_ps[e][:, :: TILES + 1, :].rearrange("q i (g m) -> q i g m", m=SEG),
-                in1=own_group[:].unsqueeze(1).unsqueeze(3).to_broadcast(shape),
+                out=own_only[:, e],
+                in0=cross_ps[e][:, :: TILES + 1, :].rearrange("q i (g m) -> q i m g", m=SEG),
+                in1=own_group[:].unsqueeze(1).unsqueeze(2).to_broadcast(shape),
                 op=ALU.mult,
+            )
+
+        used = TILES * SLOTS
+
+        def add_groups(e):
+            nc.vector.tensor_reduce(
+                out=logits[:, 0, :used].rearrange("q (i e m) -> q i e m", e=E2, m=SEG)[:, :, e, :],
+                in_=own_only[:, e],
+                axis=AXIS_X,
+                op=ALU.add,
             )
 
         regroup_weights(0)
@@ -267,35 +278,42 @@ def tile_hierarchicalsoftmoe2dblock_pb_s_kernel(tc, yn, means, w_slot2, out_0, o
             quantise_se2(e)
         for e in range(E2):
             second_matmul(e)
-        for e in range(E2):
+        zero_other_groups(0)
+        for e in range(1, E2):
             zero_other_groups(e)
-        used = TILES * SLOTS
-        nc.vector.tensor_reduce(
-            out=logits[:, 0, :used].rearrange("q (a m) -> q a m", m=SEG),
-            in_=own_only[:].rearrange("q i e g m -> q (i e) m g"),
-            axis=AXIS_X,
-            op=ALU.add,
-        )
+            add_groups(e - 1)
+        add_groups(E2 - 1)
 
         nc.vector.transpose(out=logits[:, 1, :], in_=logits[:, 0, :])
-        runs = [P, 2, TILES, TOK]
-        top = keep.tile([P, 2, TILES], F32)
-        powers = keep.tile(runs, F32)
+        runs = [P, TILES, TOK]
+        low = keep.tile([P, 2, TILES], F32)
+        powers = keep.tile([P, 2, TILES, TOK], F32)
         total = keep.tile([P, 2, TILES], F32)
-        logit_runs = logits[:, :, :used].rearrange("q h (a x) -> q h a x", x=TOK)
-        nc.vector.tensor_reduce(out=top[:], in_=logit_runs, axis=AXIS_X, op=ALU.max)
-        nc.vector.tensor_tensor(
-            out=powers[:], in0=logit_runs, in1=top[:].unsqueeze(3).to_broadcast(runs), op=ALU.subtract
-        )
-        nc.scalar.activation(out=powers[:], in_=powers[:], func=ACT.Exp)
-        nc.vector.tensor_reduce(out=total[:], in_=powers[:], axis=AXIS_X, op=ALU.add)
-        nc.vector.reciprocal(out=total[:], in_=total[:])
-        nc.vector.tensor_tensor(
-            out=shares[:, :, :used].rearrange("q h (a x) -> q h a x", x=TOK),
-            in0=powers[:],
-            in1=total[:].unsqueeze(3).to_broadcast(runs),
-            op=ALU.mult,
-        )
+        for h in range(2):
+            nc.vector.tensor_reduce(
+                out=low[:, h, :],
+                in_=logits[:, h, :used].rearrange("q (a x) -> q a x", x=TOK),
+                axis=AXIS_X,
+                op=ALU.min,
+            )
+            for a in range(TILES):
+                nc.scalar.activation(
+                    out=powers[:, h, a, :],
+                    in_=logits[:, h, a * TOK : (a + 1) * TOK],
+                    func=ACT.Exp,
+                    scale=-1.0,
+                    bias=low[:, h, a : a + 1],
+                    accum_out=total[:, h, a : a + 1],
+                )
+
+        def divide(h):
+            nc.vector.reciprocal(out=total[:, h, :], in_=total[:, h, :])
+            nc.vector.tensor_tensor(
+                out=shares[:, h, :used].rearrange("q (a x) -> q a x", x=TOK),
+                in0=powers[:, h],
+                in1=total[:, h, :].unsqueeze(2).to_broadcast(runs),
+                op=ALU.mult,
+            )
 
         def store(out, rows):
             nc.sync.dma_start(
@@ -303,7 +321,9 @@ def tile_hierarchicalsoftmoe2dblock_pb_s_kernel(tc, yn, means, w_slot2, out_0, o
                 in_=rows.rearrange("q (i p) -> q i p", p=SLOTS),
             )
 
+        divide(0)
         store(out_1, shares[:, 0, :used])
+        divide(1)
         disp = keep.tile([P, P], F32, align_bytes=64)
         nc.vector.transpose(out=disp[:], in_=shares[:, 1, :])
         store(out_0, disp[:, :used])

@@ -22,6 +22,7 @@ SEG = 4
 TOK = 16
 SLOTS = E2 * SEG
 GROUPS = 32
+HALF = D // 2
 PER_TILE = P // TOK
 TILES = GROUPS // PER_TILE
 EPS = 1e-6
@@ -39,21 +40,24 @@ def tile_hierarchicalsoftmoe2dblock_pb_s_kernel(tc, yn, means, w_slot2, out_0, o
         psum_yn = ctx.enter_context(tc.psum_pool(name="psum_yn", bufs=2))
         ctx.enter_context(tc.manual_schedule())
 
-        means_sb = keep.tile([P, D], BF16)
-        nc.sync.dma_start(out=means_sb[:], in_=means.rearrange("b g k m d -> (b g k m) d"))
-
         w_raw = {}
 
-        def load_weights(n):
+        def load_weights(n, lo, hi):
             e, k = divmod(n, E1)
-            w_raw[n] = keep.tile([P, PACK, D], BF16, name="w_raw_%d" % n)
+            raw = keep.tile([P, PACK, hi - lo], BF16, name="w_raw_%d_%d" % (n, lo))
             nc.sync.dma_start(
-                out=w_raw[n][:],
-                in_=w_slot2[k].rearrange("(t p) c -> p t c", p=P)[:, :, e * D : (e + 1) * D],
+                out=raw[:],
+                in_=w_slot2[k].rearrange("(t p) c -> p t c", p=P)[:, :, e * D + lo : e * D + hi],
             )
+            return raw
 
-        for n in range(CHUNKS):
-            load_weights(n)
+        w_raw[0] = [load_weights(0, 0, VECTOR_COLS)[:], load_weights(0, VECTOR_COLS, D)[:]]
+        for n in range(1, CHUNKS):
+            raw = load_weights(n, 0, D)
+            w_raw[n] = [raw[:, :, :VECTOR_COLS], raw[:, :, VECTOR_COLS:]]
+            if n == 1:
+                means_sb = keep.tile([P, D], BF16)
+                nc.sync.dma_start(out=means_sb[:], in_=means.rearrange("b g k m d -> (b g k m) d"))
         yn_sb = keep.tile([P, TILES, D], BF16)
         nc.sync.dma_start(
             out=yn_sb[:],
@@ -85,12 +89,14 @@ def tile_hierarchicalsoftmoe2dblock_pb_s_kernel(tc, yn, means, w_slot2, out_0, o
                 nc.tensor.transpose(turned[:, t, :], rows[:, t * P : (t + 1) * P], ident_bf[:])
             return turned
 
-        means_turned = turn(means_sb, "means_turned")
-        for kk in range(E1):
-            nc.scalar.copy(
-                out=means_grouped[:, kk].rearrange("p (a k m) t -> p a k m t", k=E1, m=SEG)[:, :, kk],
-                in_=means_turned[:].rearrange("p t (a k m) -> p a k m t", k=E1, m=SEG)[:, :, kk],
-            )
+        def group_means():
+            means_turned = turn(means_sb, "means_turned")
+            for kk in range(E1):
+                nc.scalar.copy(
+                    out=means_grouped[:, kk].rearrange("p (a k m) t -> p a k m t", k=E1, m=SEG)[:, :, kk],
+                    in_=means_turned[:].rearrange("p t (a k m) -> p a k m t", k=E1, m=SEG)[:, :, kk],
+                )
+
         means_codes = keep.tile([P, E1, P], U32, align_bytes=64)
         means_scales = keep.tile([P, E1, P], U8, align_bytes=64)
 
@@ -107,16 +113,16 @@ def tile_hierarchicalsoftmoe2dblock_pb_s_kernel(tc, yn, means, w_slot2, out_0, o
 
         yn_turned = {}
 
-        def turn_yn():
-            for half in range(2):
-                yn_turned[half] = psum_yn.tile([P, 2, 2, P], F32, name="yn_turned_%d" % half, tag="yn")
-                for j in range(2):
-                    for u in range(2):
-                        nc.tensor.transpose(
-                            yn_turned[half][:, j, u, :],
-                            yn_sb[:, 2 * half + j, :].bitcast(F32)[:, u * P : (u + 1) * P],
-                            ident_f32[:],
-                        )
+        def turn_words(out, rows):
+            for u in range(2):
+                nc.tensor.transpose(
+                    out[:, u, :], rows.bitcast(F32)[:, u * P : (u + 1) * P], ident_f32[:]
+                )
+
+        def turn_yn(half):
+            yn_turned[half] = psum_yn.tile([P, 2, 2, P], F32, name="yn_turned_%d" % half, tag="yn")
+            for j in range(2):
+                turn_words(yn_turned[half][:, j], yn_sb[:, 2 * half + j, :])
 
         def regroup_yn(half):
             words = yn_grouped[:].rearrange("p r t -> p (r t)").bitcast(F32)
@@ -133,6 +139,8 @@ def tile_hierarchicalsoftmoe2dblock_pb_s_kernel(tc, yn, means, w_slot2, out_0, o
             )
 
         w_grouped = {}
+        w_codes = {}
+        w_scales = {}
         se_ps = {}
         se2_sb = {}
         se2_turned = {}
@@ -147,39 +155,51 @@ def tile_hierarchicalsoftmoe2dblock_pb_s_kernel(tc, yn, means, w_slot2, out_0, o
             )
             nc.vector.tensor_copy(
                 out=w_grouped[n][:, :VECTOR_COLS, :].rearrange("p (c i) t -> p c t i", i=4),
-                in_=w_raw[n][:, :, :VECTOR_COLS].rearrange("p t (c i) -> p c t i", i=4),
+                in_=w_raw[n][0].rearrange("p t (c i) -> p c t i", i=4),
             )
             nc.scalar.copy(
                 out=w_grouped[n][:, VECTOR_COLS:, :].rearrange("p (c i) t -> p c t i", i=4),
-                in_=w_raw[n][:, :, VECTOR_COLS:].rearrange("p t (c i) -> p c t i", i=4),
+                in_=w_raw[n][1].rearrange("p t (c i) -> p c t i", i=4),
             )
 
-        def first_matmul(n):
-            e, k = divmod(n, E1)
-            w_codes = stage.tile([P, D], U32, align_bytes=64)
-            w_scales = stage.tile([P, D], U8, align_bytes=64)
+        def quantise_weights(n):
+            w_codes[n] = stage.tile([P, D], U32, align_bytes=64, name="w_codes_%d" % n, tag="w_codes")
+            w_scales[n] = stage.tile([P, D], U8, align_bytes=64, name="w_scales_%d" % n, tag="w_scales")
             nc.vector.quantize_mx(
-                out=w_codes[:].bitcast(FP8X4),
-                scales=w_scales[:],
+                out=w_codes[n][:].bitcast(FP8X4),
+                scales=w_scales[n][:],
                 in_=w_grouped[n][:].rearrange("p c t -> p (c t)"),
             )
-            if k == 0:
-                se_ps[e] = psum.tile([P, D], F32, name="se_ps_%d" % e, tag="bank")
+
+        def first_matmul(out, n, lo):
+            k = n % E1
             nc.tensor.matmul_mx(
-                out=se_ps[e][:],
+                out=out,
                 lhsT=means_codes[:, k, :].bitcast(FP8X4),
                 lhsT_scale=means_scales[:, k, :],
-                rhs=w_codes[:].bitcast(FP8X4),
-                rhs_scale=w_scales[:],
+                rhs=w_codes[n][:, lo:].bitcast(FP8X4),
+                rhs_scale=w_scales[n][:, lo:],
                 start=(k == 0),
                 stop=(k == E1 - 1),
             )
 
-        def normalise(e):
+        def multiply(n):
+            e = n // E1
+            if n % E1 == 0:
+                se_ps[e] = psum.tile([P, D], F32, name="se_ps_%d" % e, tag="bank")
+                if e == E2 - 1:
+                    se_ps["again"] = psum.tile([P, D], F32, name="se_ps_again", tag="bank")
+            first_matmul(se_ps[e][:], n, 0)
+            if e == E2 - 1:
+                first_matmul(se_ps["again"][:, HALF:], n, HALF)
+
+        def square(e):
             squares = stage.tile([P, D], BF16)
             nc.scalar.activation(
                 out=squares[:], in_=se_ps[e][:], func=ACT.Square, accum_out=sum_sq[:, e : e + 1]
             )
+
+        def invert(e):
             nc.scalar.activation(
                 out=inv_norm[:, e : e + 1],
                 in_=sum_sq[:, e : e + 1],
@@ -187,22 +207,34 @@ def tile_hierarchicalsoftmoe2dblock_pb_s_kernel(tc, yn, means, w_slot2, out_0, o
                 scale=1.0 / D,
                 bias=EPS / D,
             )
+
+        def scale(e):
             se2_sb[e] = stage.tile([P, D], BF16, name="se2_sb_%d" % e, tag="se2_sb")
+            cols = HALF if e == E2 - 1 else D
             nc.scalar.activation(
-                out=se2_sb[e][:].rearrange("r (u h p) -> r u h p", u=2, h=2),
-                in_=se_ps[e][:].rearrange("r (u p h) -> r u h p", u=2, h=2),
+                out=se2_sb[e][:, :cols],
+                in_=se_ps[e][:, :cols],
                 func=ACT.Copy,
                 scale=inv_norm[:, e : e + 1],
             )
+            if e == E2 - 1:
+                nc.vector.tensor_scalar_mul(
+                    se2_sb[e][:, HALF:], se_ps["again"][:, HALF:], inv_norm[:, e : e + 1]
+                )
 
         def turn_se2(e):
-            se2_turned[e] = turn(se2_sb[e], "se2_turned_%d" % e)
+            se2_turned[e] = psum.tile([P, 2, P], F32, name="se2_turned_%d" % e, tag="bank")
+            turn_words(se2_turned[e], se2_sb[e][:])
 
-        def regroup_se2(e):
-            se2_grouped[e] = stage.tile(
-                [P, P, PACK], BF16, align_bytes=64, name="se2_grouped_%d" % e, tag="se2_grouped"
+        def regroup_se2(e, copy):
+            se2_grouped[e] = keep.tile([P, P, PACK], BF16, align_bytes=64, name="se2_grouped_%d" % e)
+            copy(
+                out=se2_grouped[e][:]
+                .rearrange("p r t -> p (r t)")
+                .bitcast(F32)
+                .rearrange("p (r u) -> p r u", u=2),
+                in_=se2_turned[e][:].rearrange("p u r -> p r u"),
             )
-            nc.scalar.copy(out=se2_grouped[e][:], in_=se2_turned[e][:].rearrange("p t r -> p r t"))
 
         se2_codes = keep.tile([P, E2, P], U32, align_bytes=64)
         se2_scales = keep.tile([P, E2, P], U8, align_bytes=64)
@@ -251,31 +283,50 @@ def tile_hierarchicalsoftmoe2dblock_pb_s_kernel(tc, yn, means, w_slot2, out_0, o
             )
 
         regroup_weights(0)
-        quantise_means()
-        for n in range(1, CHUNKS):
+        regroup_weights(1)
+        quantise_weights(0)
+        group_means()
+        for n in range(2, CHUNKS):
+            done = n // E1 - 2
+            if n % E1 == 0 and n >= 4:
+                invert(done)
             regroup_weights(n)
-            first_matmul(n - 1)
-            if n % E1 == 0 and n >= 2 * E1:
-                turn_se2(n // E1 - 2)
-            if n % E1 == 1 and n >= E1 + 1:
-                normalise(n // E1 - 1)
+            if n == 2:
+                quantise_means()
+            quantise_weights(n - 1)
+            if n == 2:
+                multiply(0)
+            if n == CHUNKS - 1:
+                for half in range(2):
+                    turn_yn(half)
+            multiply(n - 1)
+            if n % E1 == 1:
+                square(n // E1 - 1)
+            elif n >= 4:
+                scale(done)
+                turn_se2(done)
 
         last = E2 - 1
-        first_matmul(CHUNKS - 1)
-        turn_yn()
+        quantise_weights(CHUNKS - 1)
+        multiply(CHUNKS - 1)
+        invert(last - 1)
+        regroup_se2(0, nc.scalar.copy)
+        scale(last - 1)
         turn_se2(last - 1)
-        regroup_se2(0)
-        normalise(last)
-        turn_se2(last)
-        for e in range(1, E2):
-            regroup_se2(e)
-        nc.scalar.activation(out=warm[:, 1:2], in_=inv_norm[:, last : last + 1], func=ACT.Exp, scale=0.0)
+        regroup_yn(0)
+        regroup_yn(1)
+        regroup_se2(1, nc.vector.tensor_copy)
         quantise_se2(0)
-        for half in range(2):
-            regroup_yn(half)
+        square(last)
+        invert(last)
+        scale(last)
+        turn_se2(last)
+        regroup_se2(last - 1, nc.scalar.copy)
         quantise_yn()
+        regroup_se2(last, nc.vector.tensor_copy)
         for e in range(1, E2):
             quantise_se2(e)
+        nc.scalar.activation(out=warm[:, 1:2], in_=inv_norm[:, last : last + 1], func=ACT.Exp, scale=0.0)
         for e in range(E2):
             second_matmul(e)
         zero_other_groups(0)

@@ -144,7 +144,9 @@ def tile_hierarchicalsoftmoe2dblock_pb_s_kernel(tc, yn, means, w_slot2, out_0, o
         se_ps = {}
         se2_sb = {}
         se2_turned = {}
-        se2_grouped = {}
+        se2_grouped = keep.tile([P, TILES, E2, PER_TILE * SEG, PACK], BF16, align_bytes=64)
+        se2_codes = keep.tile([P, TILES, P], U32, align_bytes=64)
+        se2_scales = keep.tile([P, TILES, P], U8, align_bytes=64)
         cross_ps = {}
         sum_sq = keep.tile([P, E2], F32)
         inv_norm = keep.tile([P, E2], F32)
@@ -227,57 +229,53 @@ def tile_hierarchicalsoftmoe2dblock_pb_s_kernel(tc, yn, means, w_slot2, out_0, o
             turn_words(se2_turned[e], se2_sb[e][:])
 
         def regroup_se2(e, copy):
-            se2_grouped[e] = keep.tile([P, P, PACK], BF16, align_bytes=64, name="se2_grouped_%d" % e)
+            words = se2_grouped[:].rearrange("p i e r t -> p (i e r t)").bitcast(F32)
             copy(
-                out=se2_grouped[e][:]
-                .rearrange("p r t -> p (r t)")
-                .bitcast(F32)
-                .rearrange("p (r u) -> p r u", u=2),
-                in_=se2_turned[e][:].rearrange("p u r -> p r u"),
+                out=words.rearrange("p (i e r u) -> p i e r u", i=TILES, e=E2, u=2)[:, :, e],
+                in_=se2_turned[e][:].rearrange("p u (i r) -> p i r u", i=TILES),
             )
 
-        se2_codes = keep.tile([P, E2, P], U32, align_bytes=64)
-        se2_scales = keep.tile([P, E2, P], U8, align_bytes=64)
-
-        def quantise_se2(e):
+        def quantise_se2(half):
+            tiles = slice(2 * half, 2 * half + 2)
             nc.vector.quantize_mx(
-                out=se2_codes[:, e, :].bitcast(FP8X4),
-                scales=se2_scales[:, e, :],
-                in_=se2_grouped[e][:].rearrange("p r t -> p (r t)"),
+                out=se2_codes[:, tiles].rearrange("p i c -> p (i c)").bitcast(FP8X4),
+                scales=se2_scales[:, tiles].rearrange("p i c -> p (i c)"),
+                in_=se2_grouped[:, tiles].rearrange("p i e r t -> p (i e r t)"),
             )
 
-        def second_matmul(e):
-            cross_ps[e] = psum.tile(
-                [P, TILES * TILES, PER_TILE * SEG], F32, name="cross_ps_%d" % e, tag="bank"
-            )
-            for i in range(TILES):
+        def second_matmul(half):
+            cross_ps[half] = psum.tile([P, 2, P], F32, name="cross_ps_%d" % half, tag="bank")
+            for j in range(2):
+                i = 2 * half + j
                 nc.tensor.matmul_mx(
-                    out=cross_ps[e][:, i * TILES : (i + 1) * TILES, :].rearrange("q b c -> q (b c)"),
+                    out=cross_ps[half][:, j, :],
                     lhsT=yn_codes[:, i * P : (i + 1) * P].bitcast(FP8X4),
                     lhsT_scale=yn_scales[:, i * P : (i + 1) * P],
-                    rhs=se2_codes[:, e, :].bitcast(FP8X4),
-                    rhs_scale=se2_scales[:, e, :],
+                    rhs=se2_codes[:, i, :].bitcast(FP8X4),
+                    rhs_scale=se2_scales[:, i, :],
                     start=True,
                     stop=True,
                 )
 
-        own_only = keep.tile([P, E2, TILES, SEG, PER_TILE], F32)
+        own_only = keep.tile([P, 2, 2 * E2, SEG, PER_TILE], F32)
 
-        def zero_other_groups(e):
-            shape = [P, TILES, SEG, PER_TILE]
+        def zero_other_groups(half):
+            shape = [P, 2 * E2, SEG, PER_TILE]
             nc.vector.tensor_tensor(
-                out=own_only[:, e],
-                in0=cross_ps[e][:, :: TILES + 1, :].rearrange("q i (g m) -> q i m g", m=SEG),
+                out=own_only[:, half],
+                in0=cross_ps[half][:].rearrange("q j (e g m) -> q (j e) m g", e=E2, m=SEG),
                 in1=own_group[:].unsqueeze(1).unsqueeze(2).to_broadcast(shape),
                 op=ALU.mult,
             )
 
         used = TILES * SLOTS
 
-        def add_groups(e):
+        def add_groups(half):
             nc.vector.tensor_reduce(
-                out=logits[:, 0, :used].rearrange("q (i e m) -> q i e m", e=E2, m=SEG)[:, :, e, :],
-                in_=own_only[:, e],
+                out=logits[:, 0, half * used // 2 : (half + 1) * used // 2].rearrange(
+                    "q (a m) -> q a m", m=SEG
+                ),
+                in_=own_only[:, half],
                 axis=AXIS_X,
                 op=ALU.add,
             )
@@ -316,7 +314,6 @@ def tile_hierarchicalsoftmoe2dblock_pb_s_kernel(tc, yn, means, w_slot2, out_0, o
         regroup_yn(0)
         regroup_yn(1)
         regroup_se2(1, nc.vector.tensor_copy)
-        quantise_se2(0)
         square(last)
         invert(last)
         scale(last)
@@ -324,16 +321,15 @@ def tile_hierarchicalsoftmoe2dblock_pb_s_kernel(tc, yn, means, w_slot2, out_0, o
         regroup_se2(last - 1, nc.scalar.copy)
         quantise_yn()
         regroup_se2(last, nc.vector.tensor_copy)
-        for e in range(1, E2):
-            quantise_se2(e)
+        for half in range(2):
+            quantise_se2(half)
         nc.scalar.activation(out=warm[:, 1:2], in_=inv_norm[:, last : last + 1], func=ACT.Exp, scale=0.0)
-        for e in range(E2):
-            second_matmul(e)
-        zero_other_groups(0)
-        for e in range(1, E2):
-            zero_other_groups(e)
-            add_groups(e - 1)
-        add_groups(E2 - 1)
+        for half in range(2):
+            second_matmul(half)
+        for half in range(2):
+            zero_other_groups(half)
+        for half in range(2):
+            add_groups(half)
 
         nc.vector.transpose(out=logits[:, 1, :], in_=logits[:, 0, :])
         runs = [P, TILES, TOK]

@@ -51,7 +51,7 @@ def tile_hierarchicalsoftmoe2dblock_pb_s_kernel(tc, yn, means, w_slot2, out_0, o
             )
             return raw
 
-        w_raw[0] = [load_weights(0, 0, VECTOR_COLS)[:], load_weights(0, VECTOR_COLS, D)[:]]
+        w_raw[0] = [load_weights(0, 0, HALF)[:], load_weights(0, HALF, D)[:]]
         for n in range(1, CHUNKS):
             raw = load_weights(n, 0, D)
             w_raw[n] = [raw[:, :, :VECTOR_COLS], raw[:, :, VECTOR_COLS:]]
@@ -155,12 +155,13 @@ def tile_hierarchicalsoftmoe2dblock_pb_s_kernel(tc, yn, means, w_slot2, out_0, o
             w_grouped[n] = stage.tile(
                 [P, D, PACK], BF16, align_bytes=64, name="w_grouped_%d" % n, tag="w_grouped"
             )
+            split = w_raw[n][0].shape[2]
             nc.vector.tensor_copy(
-                out=w_grouped[n][:, :VECTOR_COLS, :].rearrange("p (c i) t -> p c t i", i=4),
+                out=w_grouped[n][:, :split, :].rearrange("p (c i) t -> p c t i", i=4),
                 in_=w_raw[n][0].rearrange("p t (c i) -> p c t i", i=4),
             )
             nc.scalar.copy(
-                out=w_grouped[n][:, VECTOR_COLS:, :].rearrange("p (c i) t -> p c t i", i=4),
+                out=w_grouped[n][:, split:, :].rearrange("p (c i) t -> p c t i", i=4),
                 in_=w_raw[n][1].rearrange("p t (c i) -> p c t i", i=4),
             )
 

@@ -58,11 +58,15 @@ def tile_hierarchicalsoftmoe2dblock_pb_s_kernel(tc, yn, means, w_slot2, out_0, o
             if n == 1:
                 means_sb = keep.tile([P, D], BF16)
                 nc.sync.dma_start(out=means_sb[:], in_=means.rearrange("b g k m d -> (b g k m) d"))
-        yn_sb = keep.tile([P, TILES, D], BF16)
-        nc.sync.dma_start(
-            out=yn_sb[:],
-            in_=yn.rearrange("b g k s d -> (b g k s) d").rearrange("(i q) d -> q i d", q=P),
-        )
+        yn_sb = {}
+        for half in range(2):
+            yn_sb[half] = keep.tile([P, 2, D], BF16, name="yn_sb_%d" % half)
+            nc.sync.dma_start(
+                out=yn_sb[half][:],
+                in_=yn.rearrange("b g k s d -> (b g k s) d").rearrange("(i q) d -> q i d", q=P)[
+                    :, 2 * half : 2 * half + 2, :
+                ],
+            )
 
         ident_bf = keep.tile([P, P], BF16)
         make_identity(nc, ident_bf[:])
@@ -122,7 +126,7 @@ def tile_hierarchicalsoftmoe2dblock_pb_s_kernel(tc, yn, means, w_slot2, out_0, o
         def turn_yn(half):
             yn_turned[half] = psum_yn.tile([P, 2, 2, P], F32, name="yn_turned_%d" % half, tag="yn")
             for j in range(2):
-                turn_words(yn_turned[half][:, j], yn_sb[:, 2 * half + j, :])
+                turn_words(yn_turned[half][:, j], yn_sb[half][:, j, :])
 
         def regroup_yn(half):
             words = yn_grouped[:].rearrange("p r t -> p (r t)").bitcast(F32)
@@ -295,9 +299,6 @@ def tile_hierarchicalsoftmoe2dblock_pb_s_kernel(tc, yn, means, w_slot2, out_0, o
             quantise_weights(n - 1)
             if n == 2:
                 multiply(0)
-            if n == CHUNKS - 1:
-                for half in range(2):
-                    turn_yn(half)
             multiply(n - 1)
             if n % E1 == 1:
                 square(n // E1 - 1)
@@ -306,15 +307,17 @@ def tile_hierarchicalsoftmoe2dblock_pb_s_kernel(tc, yn, means, w_slot2, out_0, o
                 turn_se2(done)
 
         last = E2 - 1
+        turn_yn(0)
         quantise_weights(CHUNKS - 1)
         multiply(CHUNKS - 1)
+        turn_yn(1)
         invert(last - 1)
         regroup_se2(0, nc.scalar.copy)
         scale(last - 1)
         turn_se2(last - 1)
         regroup_yn(0)
-        regroup_yn(1)
         regroup_se2(1, nc.vector.tensor_copy)
+        regroup_yn(1)
         square(last)
         invert(last)
         scale(last)

@@ -27,6 +27,7 @@ PER_TILE = P // TOK
 TILES = GROUPS // PER_TILE
 EPS = 1e-6
 VECTOR_COLS = 320
+LAST_VECTOR_COLS = 352
 
 FLOPS = 2 * GROUPS * SEG * D * E2 * D + 2 * GROUPS * TOK * SLOTS * D
 
@@ -51,10 +52,8 @@ def tile_hierarchicalsoftmoe2dblock_pb_s_kernel(tc, yn, means, w_slot2, out_0, o
             )
             return raw
 
-        w_raw[0] = [load_weights(0, 0, HALF)[:], load_weights(0, HALF, D)[:]]
-        for n in range(1, CHUNKS):
-            raw = load_weights(n, 0, D)
-            w_raw[n] = [raw[:, :, :VECTOR_COLS], raw[:, :, VECTOR_COLS:]]
+        for n in range(CHUNKS):
+            w_raw[n] = load_weights(n, 0, D)
             if n == 1:
                 means_sb = keep.tile([P, D], BF16)
                 nc.sync.dma_start(out=means_sb[:], in_=means.rearrange("b g k m d -> (b g k m) d"))
@@ -82,10 +81,12 @@ def tile_hierarchicalsoftmoe2dblock_pb_s_kernel(tc, yn, means, w_slot2, out_0, o
         means_grouped = keep.tile([P, E1, P, PACK], BF16, align_bytes=64)
         nc.vector.memset(means_grouped[:], 0.0)
         own_group = keep.tile([P, PER_TILE], F32)
-        nc.vector.reduce_sum(
-            out=own_group[:], in_=ident_f32[:].rearrange("q (g s) -> q g s", s=TOK), axis=AXIS_X
-        )
-        nc.vector.tensor_scalar_mul(own_group[:], own_group[:], -1.0)
+
+        def make_own_group():
+            nc.vector.reduce_sum(
+                out=own_group[:], in_=ident_f32[:].rearrange("q (g s) -> q g s", s=TOK), axis=AXIS_X
+            )
+            nc.vector.tensor_scalar_mul(own_group[:], own_group[:], -1.0)
 
         def turn(rows, name):
             turned = psum.tile([P, PACK, P], BF16, name=name, tag="bank")
@@ -159,14 +160,14 @@ def tile_hierarchicalsoftmoe2dblock_pb_s_kernel(tc, yn, means, w_slot2, out_0, o
             w_grouped[n] = stage.tile(
                 [P, D, PACK], BF16, align_bytes=64, name="w_grouped_%d" % n, tag="w_grouped"
             )
-            split = w_raw[n][0].shape[2]
+            split = LAST_VECTOR_COLS if n == CHUNKS - 1 else VECTOR_COLS
             nc.vector.tensor_copy(
                 out=w_grouped[n][:, :split, :].rearrange("p (c i) t -> p c t i", i=4),
-                in_=w_raw[n][0].rearrange("p t (c i) -> p c t i", i=4),
+                in_=w_raw[n][:, :, :split].rearrange("p t (c i) -> p c t i", i=4),
             )
             nc.scalar.copy(
                 out=w_grouped[n][:, split:, :].rearrange("p (c i) t -> p c t i", i=4),
-                in_=w_raw[n][1].rearrange("p t (c i) -> p c t i", i=4),
+                in_=w_raw[n][:, :, split:].rearrange("p t (c i) -> p c t i", i=4),
             )
 
         def quantise_weights(n):
@@ -286,6 +287,7 @@ def tile_hierarchicalsoftmoe2dblock_pb_s_kernel(tc, yn, means, w_slot2, out_0, o
             )
 
         regroup_weights(0)
+        make_own_group()
         regroup_weights(1)
         quantise_weights(0)
         group_means()
@@ -293,13 +295,18 @@ def tile_hierarchicalsoftmoe2dblock_pb_s_kernel(tc, yn, means, w_slot2, out_0, o
             done = n // E1 - 2
             if n % E1 == 0 and n >= 4:
                 invert(done)
-            regroup_weights(n)
-            if n == 2:
-                quantise_means()
-            quantise_weights(n - 1)
-            if n == 2:
-                multiply(0)
-            multiply(n - 1)
+            if n == CHUNKS - 1:
+                quantise_weights(n - 1)
+                multiply(n - 1)
+                regroup_weights(n)
+            else:
+                regroup_weights(n)
+                if n == 2:
+                    quantise_means()
+                quantise_weights(n - 1)
+                if n == 2:
+                    multiply(0)
+                multiply(n - 1)
             if n % E1 == 1:
                 square(n // E1 - 1)
             elif n >= 4:

@@ -37,8 +37,9 @@ def tile_hierarchicalsoftmoe2dblock_pb_s_kernel(tc, yn, means, w_slot2, out_0, o
     with ExitStack() as ctx:
         keep = ctx.enter_context(tc.tile_pool(name="keep", bufs=1))
         stage = ctx.enter_context(tc.tile_pool(name="stage", bufs=3))
-        psum = ctx.enter_context(tc.psum_pool(name="psum", bufs=6))
+        psum = ctx.enter_context(tc.psum_pool(name="psum", bufs=5))
         psum_yn = ctx.enter_context(tc.psum_pool(name="psum_yn", bufs=2))
+        psum_spare = ctx.enter_context(tc.psum_pool(name="psum_spare", bufs=1))
         ctx.enter_context(tc.manual_schedule())
 
         w_raw = {}
@@ -74,10 +75,10 @@ def tile_hierarchicalsoftmoe2dblock_pb_s_kernel(tc, yn, means, w_slot2, out_0, o
         warm = keep.tile([P, 2], F32)
         nc.vector.memset(warm[:], 1.0)
         nc.scalar.activation(out=warm[:, 1:2], in_=warm[:, 0:1], func=ACT.Abs_reciprocal_sqrt)
-        logits = keep.tile([P, 2, P], F32, align_bytes=64)
-        nc.vector.memset(logits[:], 0.0)
-        shares = keep.tile([P, 2, P], F32, align_bytes=64)
-        nc.vector.memset(shares[:], 0.0)
+        used = TILES * SLOTS
+        block = 32
+        logits = keep.tile([P, 2, used], F32, align_bytes=64)
+        shares = keep.tile([P, 2, used], F32, align_bytes=64)
         means_grouped = keep.tile([P, E1, P, PACK], BF16, align_bytes=64)
         nc.vector.memset(means_grouped[:], 0.0)
         own_group = keep.tile([P, PER_TILE], F32)
@@ -153,81 +154,116 @@ def tile_hierarchicalsoftmoe2dblock_pb_s_kernel(tc, yn, means, w_slot2, out_0, o
         se2_codes = keep.tile([P, TILES, P], U32, align_bytes=64)
         se2_scales = keep.tile([P, TILES, P], U8, align_bytes=64)
         cross_ps = {}
-        sum_sq = keep.tile([P, E2], F32)
+        sum_sq = keep.tile([P, E2 + 1], F32)
+        part_norm = keep.tile([P, 1], F32)
         inv_norm = keep.tile([P, E2], F32)
+
+        def regroup_share(n, copy, lo, hi):
+            copy(
+                out=w_grouped[n][:, lo:hi, :].rearrange("p (c i) t -> p c t i", i=4),
+                in_=w_raw[n][:, :, lo:hi].rearrange("p t (c i) -> p c t i", i=4),
+            )
 
         def regroup_weights(n):
             w_grouped[n] = stage.tile(
                 [P, D, PACK], BF16, align_bytes=64, name="w_grouped_%d" % n, tag="w_grouped"
             )
-            split = LAST_VECTOR_COLS if n == CHUNKS - 1 else VECTOR_COLS
-            nc.vector.tensor_copy(
-                out=w_grouped[n][:, :split, :].rearrange("p (c i) t -> p c t i", i=4),
-                in_=w_raw[n][:, :, :split].rearrange("p t (c i) -> p c t i", i=4),
-            )
-            nc.scalar.copy(
-                out=w_grouped[n][:, split:, :].rearrange("p (c i) t -> p c t i", i=4),
-                in_=w_raw[n][:, :, split:].rearrange("p t (c i) -> p c t i", i=4),
-            )
+            regroup_share(n, nc.vector.tensor_copy, 0, HALF if n == CHUNKS - 1 else VECTOR_COLS)
+            if n < CHUNKS - 1:
+                regroup_share(n, nc.scalar.copy, VECTOR_COLS, D)
 
-        def quantise_weights(n):
+        def regroup_rest():
+            regroup_share(CHUNKS - 1, nc.vector.tensor_copy, HALF, LAST_VECTOR_COLS)
+            regroup_share(CHUNKS - 1, nc.scalar.copy, LAST_VECTOR_COLS, D)
+
+        def quantise_weights(n, parts=1):
             w_codes[n] = stage.tile([P, D], U32, align_bytes=64, name="w_codes_%d" % n, tag="w_codes")
             w_scales[n] = stage.tile([P, D], U8, align_bytes=64, name="w_scales_%d" % n, tag="w_scales")
-            nc.vector.quantize_mx(
-                out=w_codes[n][:].bitcast(FP8X4),
-                scales=w_scales[n][:],
-                in_=w_grouped[n][:].rearrange("p c t -> p (c t)"),
-            )
-
-        def first_matmul(out, n, lo):
-            k = n % E1
-            nc.tensor.matmul_mx(
-                out=out,
-                lhsT=means_codes[:, k, :].bitcast(FP8X4),
-                lhsT_scale=means_scales[:, k, :],
-                rhs=w_codes[n][:, lo:].bitcast(FP8X4),
-                rhs_scale=w_scales[n][:, lo:],
-                start=(k == 0),
-                stop=(k == E1 - 1),
-            )
+            for u in range(parts):
+                cols = slice(u * D // parts, (u + 1) * D // parts)
+                nc.vector.quantize_mx(
+                    out=w_codes[n][:, cols].bitcast(FP8X4),
+                    scales=w_scales[n][:, cols],
+                    in_=w_grouped[n][:, cols, :].rearrange("p c t -> p (c t)"),
+                )
 
         def multiply(n):
-            e = n // E1
-            if n % E1 == 0:
-                se_ps[e] = psum.tile([P, D], F32, name="se_ps_%d" % e, tag="bank")
-                if e == E2 - 1:
-                    se_ps["again"] = psum.tile([P, D], F32, name="se_ps_again", tag="bank")
-            first_matmul(se_ps[e][:], n, 0)
-            if e == E2 - 1:
-                first_matmul(se_ps["again"][:, HALF:], n, HALF)
+            e, k = divmod(n, E1)
+            width = HALF if e == E2 - 1 else D
+            if k == 0:
+                se_ps[e] = [
+                    psum.tile([P, width], F32, name="se_ps_%d_%d" % (e, u), tag="bank")
+                    for u in range(D // width)
+                ]
+            for u, out in enumerate(se_ps[e]):
+                cols = slice(u * width, (u + 1) * width)
+                nc.tensor.matmul_mx(
+                    out=out[:],
+                    lhsT=means_codes[:, k, :].bitcast(FP8X4),
+                    lhsT_scale=means_scales[:, k, :],
+                    rhs=w_codes[n][:, cols].bitcast(FP8X4),
+                    rhs_scale=w_scales[n][:, cols],
+                    start=(k == 0),
+                    stop=(k == E1 - 1),
+                )
+
+        spare = psum_spare.tile([P, D], F32)
+
+        def keep_busy(n, times):
+            k = n % E1
+            for i in range(times):
+                nc.tensor.matmul_mx(
+                    out=spare[:],
+                    lhsT=means_codes[:, k, :].bitcast(FP8X4),
+                    lhsT_scale=means_scales[:, k, :],
+                    rhs=w_codes[n][:].bitcast(FP8X4),
+                    rhs_scale=w_scales[n][:],
+                    start=True,
+                    stop=True,
+                )
 
         def square(e):
-            squares = stage.tile([P, D], BF16)
-            nc.scalar.activation(
-                out=squares[:], in_=se_ps[e][:], func=ACT.Square, accum_out=sum_sq[:, e : e + 1]
-            )
+            for u, bank in enumerate(se_ps[e]):
+                squares = stage.tile([P, D], BF16)
+                nc.scalar.activation(
+                    out=squares[:, : bank.shape[1]],
+                    in_=bank[:],
+                    func=ACT.Square,
+                    accum_out=sum_sq[:, e + u : e + u + 1],
+                )
 
         def invert(e):
+            bias = EPS / D
+            if len(se_ps[e]) == 2:
+                nc.scalar.activation(
+                    out=part_norm[:],
+                    in_=sum_sq[:, e : e + 1],
+                    func=ACT.Identity,
+                    scale=1.0 / D,
+                    bias=EPS / D,
+                )
+                bias = part_norm[:]
+            last_sum = e + len(se_ps[e]) - 1
             nc.scalar.activation(
                 out=inv_norm[:, e : e + 1],
-                in_=sum_sq[:, e : e + 1],
+                in_=sum_sq[:, last_sum : last_sum + 1],
                 func=ACT.Abs_reciprocal_sqrt,
                 scale=1.0 / D,
-                bias=EPS / D,
+                bias=bias,
             )
 
         def scale(e):
             se2_sb[e] = stage.tile([P, D], BF16, name="se2_sb_%d" % e, tag="se2_sb")
-            cols = HALF if e == E2 - 1 else D
+            bank = se_ps[e][0]
             nc.scalar.activation(
-                out=se2_sb[e][:, :cols],
-                in_=se_ps[e][:, :cols],
+                out=se2_sb[e][:, : bank.shape[1]],
+                in_=bank[:],
                 func=ACT.Copy,
                 scale=inv_norm[:, e : e + 1],
             )
-            if e == E2 - 1:
+            if len(se_ps[e]) == 2:
                 nc.vector.tensor_scalar_mul(
-                    se2_sb[e][:, HALF:], se_ps["again"][:, HALF:], inv_norm[:, e : e + 1]
+                    se2_sb[e][:, HALF:], se_ps[e][1][:], inv_norm[:, e : e + 1]
                 )
 
         def turn_se2(e):
@@ -236,10 +272,13 @@ def tile_hierarchicalsoftmoe2dblock_pb_s_kernel(tc, yn, means, w_slot2, out_0, o
 
         def regroup_se2(e, copy):
             words = se2_grouped[:].rearrange("p i e r t -> p (i e r t)").bitcast(F32)
-            copy(
-                out=words.rearrange("p (i e r u) -> p i e r u", i=TILES, e=E2, u=2)[:, :, e],
-                in_=se2_turned[e][:].rearrange("p u (i r) -> p i r u", i=TILES),
-            )
+            parts = 2 if e == E2 - 1 else 1
+            for h in range(parts):
+                tiles = slice(h * TILES // parts, (h + 1) * TILES // parts)
+                copy(
+                    out=words.rearrange("p (i e r u) -> p i e r u", i=TILES, e=E2, u=2)[:, tiles, e],
+                    in_=se2_turned[e][:].rearrange("p u (i r) -> p i r u", i=TILES)[:, tiles],
+                )
 
         def quantise_se2(half):
             tiles = slice(2 * half, 2 * half + 2)
@@ -274,8 +313,6 @@ def tile_hierarchicalsoftmoe2dblock_pb_s_kernel(tc, yn, means, w_slot2, out_0, o
                 op=ALU.mult,
             )
 
-        used = TILES * SLOTS
-
         def add_groups(half):
             nc.vector.tensor_reduce(
                 out=logits[:, 0, half * used // 2 : (half + 1) * used // 2].rearrange(
@@ -286,6 +323,10 @@ def tile_hierarchicalsoftmoe2dblock_pb_s_kernel(tc, yn, means, w_slot2, out_0, o
                 op=ALU.add,
             )
 
+        def turn_block(out, rows, half):
+            cols = slice(half * block, (half + 1) * block)
+            nc.vector.transpose(out=out[:, cols], in_=rows[:, cols])
+
         regroup_weights(0)
         make_own_group()
         regroup_weights(1)
@@ -295,18 +336,17 @@ def tile_hierarchicalsoftmoe2dblock_pb_s_kernel(tc, yn, means, w_slot2, out_0, o
             done = n // E1 - 2
             if n % E1 == 0 and n >= 4:
                 invert(done)
+            regroup_weights(n)
+            if n == 2:
+                quantise_means()
+            quantise_weights(n - 1)
+            if n == 2:
+                multiply(0)
+            multiply(n - 1)
             if n == CHUNKS - 1:
-                quantise_weights(n - 1)
-                multiply(n - 1)
-                regroup_weights(n)
-            else:
-                regroup_weights(n)
-                if n == 2:
-                    quantise_means()
-                quantise_weights(n - 1)
-                if n == 2:
-                    multiply(0)
-                multiply(n - 1)
+                regroup_rest()
+            if n < CHUNKS - 1:
+                keep_busy(n - 1, 1)
             if n % E1 == 1:
                 square(n // E1 - 1)
             elif n >= 4:
@@ -315,11 +355,12 @@ def tile_hierarchicalsoftmoe2dblock_pb_s_kernel(tc, yn, means, w_slot2, out_0, o
 
         last = E2 - 1
         turn_yn(0)
-        quantise_weights(CHUNKS - 1)
+        quantise_weights(CHUNKS - 1, parts=2)
         multiply(CHUNKS - 1)
         turn_yn(1)
+        keep_busy(CHUNKS - 1, 2)
         invert(last - 1)
-        regroup_se2(0, nc.scalar.copy)
+        regroup_se2(0, nc.vector.tensor_copy)
         scale(last - 1)
         turn_se2(last - 1)
         regroup_yn(0)
@@ -329,6 +370,7 @@ def tile_hierarchicalsoftmoe2dblock_pb_s_kernel(tc, yn, means, w_slot2, out_0, o
         invert(last)
         scale(last)
         turn_se2(last)
+        keep_busy(CHUNKS - 1, 2)
         regroup_se2(last - 1, nc.scalar.copy)
         quantise_yn()
         regroup_se2(last, nc.vector.tensor_copy)
@@ -342,36 +384,43 @@ def tile_hierarchicalsoftmoe2dblock_pb_s_kernel(tc, yn, means, w_slot2, out_0, o
         for half in range(2):
             add_groups(half)
 
-        nc.vector.transpose(out=logits[:, 1, :], in_=logits[:, 0, :])
-        runs = [P, TILES, TOK]
         low = keep.tile([P, 2, TILES], F32)
         powers = keep.tile([P, 2, TILES, TOK], F32)
         total = keep.tile([P, 2, TILES], F32)
-        for h in range(2):
+        logit_runs = logits[:].rearrange("q h (a x) -> q h a x", x=TOK)
+        share_runs = shares[:].rearrange("q h (a x) -> q h a x", x=TOK)
+
+        def exponentials(h, half):
+            two = slice(2 * half, 2 * half + 2)
             nc.vector.tensor_reduce(
-                out=low[:, h, :],
-                in_=logits[:, h, :used].rearrange("q (a x) -> q a x", x=TOK),
-                axis=AXIS_X,
-                op=ALU.min,
+                out=low[:, h, two], in_=logit_runs[:, h, two, :], axis=AXIS_X, op=ALU.min
             )
-            for a in range(TILES):
+            for a in (2 * half, 2 * half + 1):
                 nc.scalar.activation(
                     out=powers[:, h, a, :],
-                    in_=logits[:, h, a * TOK : (a + 1) * TOK],
+                    in_=logit_runs[:, h, a, :],
                     func=ACT.Exp,
                     scale=-1.0,
                     bias=low[:, h, a : a + 1],
                     accum_out=total[:, h, a : a + 1],
                 )
 
-        def divide(h):
+        for half in range(2):
+            turn_block(logits[:, 1], logits[:, 0], half)
+            exponentials(0, half)
+        for half in range(2):
+            exponentials(1, half)
+
+        def divide(h, parts):
             nc.vector.reciprocal(out=total[:, h, :], in_=total[:, h, :])
-            nc.vector.tensor_tensor(
-                out=shares[:, h, :used].rearrange("q (a x) -> q a x", x=TOK),
-                in0=powers[:, h],
-                in1=total[:, h, :].unsqueeze(2).to_broadcast(runs),
-                op=ALU.mult,
-            )
+            for part in range(parts):
+                tiles = slice(part * TILES // parts, (part + 1) * TILES // parts)
+                nc.vector.tensor_tensor(
+                    out=share_runs[:, h, tiles, :],
+                    in0=powers[:, h, tiles, :],
+                    in1=total[:, h, tiles].unsqueeze(2).to_broadcast([P, TILES // parts, TOK]),
+                    op=ALU.mult,
+                )
 
         def store(out, rows):
             nc.sync.dma_start(
@@ -379,9 +428,10 @@ def tile_hierarchicalsoftmoe2dblock_pb_s_kernel(tc, yn, means, w_slot2, out_0, o
                 in_=rows.rearrange("q (i p) -> q i p", p=SLOTS),
             )
 
-        divide(0)
-        store(out_1, shares[:, 0, :used])
-        divide(1)
-        disp = keep.tile([P, P], F32, align_bytes=64)
-        nc.vector.transpose(out=disp[:], in_=shares[:, 1, :])
-        store(out_0, disp[:, :used])
+        divide(0, 1)
+        store(out_1, shares[:, 0, :])
+        divide(1, 2)
+        disp = keep.tile([P, used], F32, align_bytes=64)
+        for half in range(2):
+            turn_block(disp, shares[:, 1], half)
+        store(out_0, disp[:])

from contextlib import ExitStack

import concourse.mybir as mybir
from concourse.masks import make_identity

BF16 = mybir.dt.bfloat16
F32 = mybir.dt.float32
U32 = mybir.dt.uint32
U8 = mybir.dt.uint8
FP8X4 = mybir.dt.float8_e4m3fn_x4
ACT = mybir.ActivationFunctionType
ALU = mybir.AluOpType
AXIS_X = mybir.AxisListType.X

P = 128
PACK = 4
D = P * PACK
E1 = 2
E2 = 4
CHUNKS = E2 * E1
SEG = 4
TOK = 16
SLOTS = E2 * SEG
GROUPS = 32
HALF = D // 2
PER_TILE = P // TOK
TILES = GROUPS // PER_TILE
EPS = 1e-6
VECTOR_COLS = 320
LAST_VECTOR_COLS = 352

FLOPS = 2 * GROUPS * SEG * D * E2 * D + 2 * GROUPS * TOK * SLOTS * D


def tile_hierarchicalsoftmoe2dblock_pb_s_kernel(tc, yn, means, w_slot2, out_0, out_1):
    nc = tc.nc
    with ExitStack() as ctx:
        keep = ctx.enter_context(tc.tile_pool(name="keep", bufs=1))
        stage = ctx.enter_context(tc.tile_pool(name="stage", bufs=3))
        psum = ctx.enter_context(tc.psum_pool(name="psum", bufs=5))
        psum_yn = ctx.enter_context(tc.psum_pool(name="psum_yn", bufs=2))
        psum_spare = ctx.enter_context(tc.psum_pool(name="psum_spare", bufs=1))
        ctx.enter_context(tc.manual_schedule())

        w_raw = {}

        def load_weights(n, lo, hi):
            e, k = divmod(n, E1)
            raw = keep.tile([P, PACK, hi - lo], BF16, name="w_raw_%d_%d" % (n, lo))
            nc.sync.dma_start(
                out=raw[:],
                in_=w_slot2[k].rearrange("(t p) c -> p t c", p=P)[:, :, e * D + lo : e * D + hi],
            )
            return raw

        for n in range(CHUNKS):
            w_raw[n] = load_weights(n, 0, D)
            if n == 1:
                means_sb = keep.tile([P, D], BF16)
                nc.sync.dma_start(out=means_sb[:], in_=means.rearrange("b g k m d -> (b g k m) d"))
        yn_sb = {}
        for half in range(2):
            yn_sb[half] = keep.tile([P, 2, D], BF16, name="yn_sb_%d" % half)
            nc.sync.dma_start(
                out=yn_sb[half][:],
                in_=yn.rearrange("b g k s d -> (b g k s) d").rearrange("(i q) d -> q i d", q=P)[
                    :, 2 * half : 2 * half + 2, :
                ],
            )

        ident_bf = keep.tile([P, P], BF16)
        make_identity(nc, ident_bf[:])
        ident_f32 = keep.tile([P, P], F32)
        make_identity(nc, ident_f32[:])
        warm = keep.tile([P, 2], F32)
        nc.vector.memset(warm[:], 1.0)
        nc.scalar.activation(out=warm[:, 1:2], in_=warm[:, 0:1], func=ACT.Abs_reciprocal_sqrt)
        used = TILES * SLOTS
        block = 32
        logits = keep.tile([P, 2, used], F32, align_bytes=64)
        shares = keep.tile([P, 2, used], F32, align_bytes=64)
        means_grouped = keep.tile([P, E1, P, PACK], BF16, align_bytes=64)
        nc.vector.memset(means_grouped[:], 0.0)
        own_group = keep.tile([P, PER_TILE], F32)

        def make_own_group():
            nc.vector.reduce_sum(
                out=own_group[:], in_=ident_f32[:].rearrange("q (g s) -> q g s", s=TOK), axis=AXIS_X
            )
            nc.vector.tensor_scalar_mul(own_group[:], own_group[:], -1.0)

        def turn(rows, name):
            turned = psum.tile([P, PACK, P], BF16, name=name, tag="bank")
            for t in range(PACK):
                nc.tensor.transpose(turned[:, t, :], rows[:, t * P : (t + 1) * P], ident_bf[:])
            return turned

        def group_means():
            means_turned = turn(means_sb, "means_turned")
            for kk in range(E1):
                nc.scalar.copy(
                    out=means_grouped[:, kk].rearrange("p (a k m) t -> p a k m t", k=E1, m=SEG)[:, :, kk],
                    in_=means_turned[:].rearrange("p t (a k m) -> p a k m t", k=E1, m=SEG)[:, :, kk],
                )

        means_codes = keep.tile([P, E1, P], U32, align_bytes=64)
        means_scales = keep.tile([P, E1, P], U8, align_bytes=64)

        def quantise_means():
            nc.vector.quantize_mx(
                out=means_codes[:].rearrange("p k r -> p (k r)").bitcast(FP8X4),
                scales=means_scales[:].rearrange("p k r -> p (k r)"),
                in_=means_grouped[:].rearrange("p k r t -> p (k r t)"),
            )

        yn_grouped = keep.tile([P, TILES * P, PACK], BF16, align_bytes=64)
        yn_codes = keep.tile([P, TILES * P], U32, align_bytes=64)
        yn_scales = keep.tile([P, TILES * P], U8, align_bytes=64)

        yn_turned = {}

        def turn_words(out, rows):
            for u in range(2):
                nc.tensor.transpose(
                    out[:, u, :], rows.bitcast(F32)[:, u * P : (u + 1) * P], ident_f32[:]
                )

        def turn_yn(half):
            yn_turned[half] = psum_yn.tile([P, 2, 2, P], F32, name="yn_turned_%d" % half, tag="yn")
            for j in range(2):
                turn_words(yn_turned[half][:, j], yn_sb[half][:, j, :])

        def regroup_yn(half):
            words = yn_grouped[:].rearrange("p r t -> p (r t)").bitcast(F32)
            nc.vector.tensor_copy(
                out=words[:, half * D : (half + 1) * D].rearrange("p (j r u) -> p j r u", j=2, u=2),
                in_=yn_turned[half][:].rearrange("p j u r -> p j r u"),
            )

        def quantise_yn():
            nc.vector.quantize_mx(
                out=yn_codes[:].bitcast(FP8X4),
                scales=yn_scales[:],
                in_=yn_grouped[:].rearrange("p r t -> p (r t)"),
            )

        w_grouped = {}
        w_codes = {}
        w_scales = {}
        se_ps = {}
        se2_sb = {}
        se2_turned = {}
        se2_grouped = keep.tile([P, TILES, E2, PER_TILE * SEG, PACK], BF16, align_bytes=64)
        se2_codes = keep.tile([P, TILES, P], U32, align_bytes=64)
        se2_scales = keep.tile([P, TILES, P], U8, align_bytes=64)
        cross_ps = {}
        sum_sq = keep.tile([P, E2 + 1], F32)
        part_norm = keep.tile([P, 1], F32)
        inv_norm = keep.tile([P, E2], F32)

        def regroup_share(n, copy, lo, hi):
            copy(
                out=w_grouped[n][:, lo:hi, :].rearrange("p (c i) t -> p c t i", i=4),
                in_=w_raw[n][:, :, lo:hi].rearrange("p t (c i) -> p c t i", i=4),
            )

        def regroup_weights(n):
            w_grouped[n] = stage.tile(
                [P, D, PACK], BF16, align_bytes=64, name="w_grouped_%d" % n, tag="w_grouped"
            )
            regroup_share(n, nc.vector.tensor_copy, 0, HALF if n == CHUNKS - 1 else VECTOR_COLS)
            if n < CHUNKS - 1:
                regroup_share(n, nc.scalar.copy, VECTOR_COLS, D)

        def regroup_rest():
            regroup_share(CHUNKS - 1, nc.vector.tensor_copy, HALF, LAST_VECTOR_COLS)
            regroup_share(CHUNKS - 1, nc.scalar.copy, LAST_VECTOR_COLS, D)

        def quantise_weights(n, parts=1):
            w_codes[n] = stage.tile([P, D], U32, align_bytes=64, name="w_codes_%d" % n, tag="w_codes")
            w_scales[n] = stage.tile([P, D], U8, align_bytes=64, name="w_scales_%d" % n, tag="w_scales")
            for u in range(parts):
                cols = slice(u * D // parts, (u + 1) * D // parts)
                nc.vector.quantize_mx(
                    out=w_codes[n][:, cols].bitcast(FP8X4),
                    scales=w_scales[n][:, cols],
                    in_=w_grouped[n][:, cols, :].rearrange("p c t -> p (c t)"),
                )

        def multiply(n):
            e, k = divmod(n, E1)
            width = HALF if e == E2 - 1 else D
            if k == 0:
                se_ps[e] = [
                    psum.tile([P, width], F32, name="se_ps_%d_%d" % (e, u), tag="bank")
                    for u in range(D // width)
                ]
            for u, out in enumerate(se_ps[e]):
                cols = slice(u * width, (u + 1) * width)
                nc.tensor.matmul_mx(
                    out=out[:],
                    lhsT=means_codes[:, k, :].bitcast(FP8X4),
                    lhsT_scale=means_scales[:, k, :],
                    rhs=w_codes[n][:, cols].bitcast(FP8X4),
                    rhs_scale=w_scales[n][:, cols],
                    start=(k == 0),
                    stop=(k == E1 - 1),
                )

        spare = psum_spare.tile([P, D], F32)

        def keep_busy(n, times):
            k = n % E1
            for i in range(times):
                nc.tensor.matmul_mx(
                    out=spare[:],
                    lhsT=means_codes[:, k, :].bitcast(FP8X4),
                    lhsT_scale=means_scales[:, k, :],
                    rhs=w_codes[n][:].bitcast(FP8X4),
                    rhs_scale=w_scales[n][:],
                    start=True,
                    stop=True,
                )

        def square(e):
            for u, bank in enumerate(se_ps[e]):
                squares = stage.tile([P, D], BF16)
                nc.scalar.activation(
                    out=squares[:, : bank.shape[1]],
                    in_=bank[:],
                    func=ACT.Square,
                    accum_out=sum_sq[:, e + u : e + u + 1],
                )

        def invert(e):
            bias = EPS / D
            if len(se_ps[e]) == 2:
                nc.scalar.activation(
                    out=part_norm[:],
                    in_=sum_sq[:, e : e + 1],
                    func=ACT.Identity,
                    scale=1.0 / D,
                    bias=EPS / D,
                )
                bias = part_norm[:]
            last_sum = e + len(se_ps[e]) - 1
            nc.scalar.activation(
                out=inv_norm[:, e : e + 1],
                in_=sum_sq[:, last_sum : last_sum + 1],
                func=ACT.Abs_reciprocal_sqrt,
                scale=1.0 / D,
                bias=bias,
            )

        def scale(e):
            se2_sb[e] = stage.tile([P, D], BF16, name="se2_sb_%d" % e, tag="se2_sb")
            bank = se_ps[e][0]
            nc.scalar.activation(
                out=se2_sb[e][:, : bank.shape[1]],
                in_=bank[:],
                func=ACT.Copy,
                scale=inv_norm[:, e : e + 1],
            )
            if len(se_ps[e]) == 2:
                nc.vector.tensor_scalar_mul(
                    se2_sb[e][:, HALF:], se_ps[e][1][:], inv_norm[:, e : e + 1]
                )

        def turn_se2(e):
            se2_turned[e] = psum.tile([P, 2, P], F32, name="se2_turned_%d" % e, tag="bank")
            turn_words(se2_turned[e], se2_sb[e][:])

        def regroup_se2(e, copy):
            words = se2_grouped[:].rearrange("p i e r t -> p (i e r t)").bitcast(F32)
            parts = 2 if e == E2 - 1 else 1
            for h in range(parts):
                tiles = slice(h * TILES // parts, (h + 1) * TILES // parts)
                copy(
                    out=words.rearrange("p (i e r u) -> p i e r u", i=TILES, e=E2, u=2)[:, tiles, e],
                    in_=se2_turned[e][:].rearrange("p u (i r) -> p i r u", i=TILES)[:, tiles],
                )

        def quantise_se2(half):
            tiles = slice(2 * half, 2 * half + 2)
            nc.vector.quantize_mx(
                out=se2_codes[:, tiles].rearrange("p i c -> p (i c)").bitcast(FP8X4),
                scales=se2_scales[:, tiles].rearrange("p i c -> p (i c)"),
                in_=se2_grouped[:, tiles].rearrange("p i e r t -> p (i e r t)"),
            )

        def second_matmul(half):
            cross_ps[half] = psum.tile([P, 2, P], F32, name="cross_ps_%d" % half, tag="bank")
            for j in range(2):
                i = 2 * half + j
                nc.tensor.matmul_mx(
                    out=cross_ps[half][:, j, :],
                    lhsT=yn_codes[:, i * P : (i + 1) * P].bitcast(FP8X4),
                    lhsT_scale=yn_scales[:, i * P : (i + 1) * P],
                    rhs=se2_codes[:, i, :].bitcast(FP8X4),
                    rhs_scale=se2_scales[:, i, :],
                    start=True,
                    stop=True,
                )

        own_only = keep.tile([P, 2, 2 * E2, SEG, PER_TILE], F32)

        def zero_other_groups(half):
            shape = [P, 2 * E2, SEG, PER_TILE]
            nc.vector.tensor_tensor(
                out=own_only[:, half],
                in0=cross_ps[half][:].rearrange("q j (e g m) -> q (j e) m g", e=E2, m=SEG),
                in1=own_group[:].unsqueeze(1).unsqueeze(2).to_broadcast(shape),
                op=ALU.mult,
            )

        def add_groups(half):
            nc.vector.tensor_reduce(
                out=logits[:, 0, half * used // 2 : (half + 1) * used // 2].rearrange(
                    "q (a m) -> q a m", m=SEG
                ),
                in_=own_only[:, half],
                axis=AXIS_X,
                op=ALU.add,
            )

        def turn_block(out, rows, half):
            cols = slice(half * block, (half + 1) * block)
            nc.vector.transpose(out=out[:, cols], in_=rows[:, cols])

        regroup_weights(0)
        make_own_group()
        regroup_weights(1)
        quantise_weights(0)
        group_means()
        for n in range(2, CHUNKS):
            done = n // E1 - 2
            if n % E1 == 0 and n >= 4:
                invert(done)
            regroup_weights(n)
            if n == 2:
                quantise_means()
            quantise_weights(n - 1)
            if n == 2:
                multiply(0)
            multiply(n - 1)
            if n == CHUNKS - 1:
                regroup_rest()
            if n < CHUNKS - 1:
                keep_busy(n - 1, 1)
            if n % E1 == 1:
                square(n // E1 - 1)
            elif n >= 4:
                scale(done)
                turn_se2(done)

        last = E2 - 1
        turn_yn(0)
        quantise_weights(CHUNKS - 1, parts=2)
        multiply(CHUNKS - 1)
        turn_yn(1)
        keep_busy(CHUNKS - 1, 2)
        invert(last - 1)
        regroup_se2(0, nc.vector.tensor_copy)
        scale(last - 1)
        turn_se2(last - 1)
        regroup_yn(0)
        regroup_se2(1, nc.vector.tensor_copy)
        regroup_yn(1)
        square(last)
        invert(last)
        scale(last)
        turn_se2(last)
        keep_busy(CHUNKS - 1, 2)
        regroup_se2(last - 1, nc.scalar.copy)
        quantise_yn()
        regroup_se2(last, nc.vector.tensor_copy)
        for half in range(2):
            quantise_se2(half)
        nc.scalar.activation(out=warm[:, 1:2], in_=inv_norm[:, last : last + 1], func=ACT.Exp, scale=0.0)
        for half in range(2):
            second_matmul(half)
        for half in range(2):
            zero_other_groups(half)
        for half in range(2):
            add_groups(half)

        low = keep.tile([P, 2, TILES], F32)
        powers = keep.tile([P, 2, TILES, TOK], F32)
        total = keep.tile([P, 2, TILES], F32)
        logit_runs = logits[:].rearrange("q h (a x) -> q h a x", x=TOK)
        share_runs = shares[:].rearrange("q h (a x) -> q h a x", x=TOK)

        def exponentials(h, half):
            two = slice(2 * half, 2 * half + 2)
            nc.vector.tensor_reduce(
                out=low[:, h, two], in_=logit_runs[:, h, two, :], axis=AXIS_X, op=ALU.min
            )
            for a in (2 * half, 2 * half + 1):
                nc.scalar.activation(
                    out=powers[:, h, a, :],
                    in_=logit_runs[:, h, a, :],
                    func=ACT.Exp,
                    scale=-1.0,
                    bias=low[:, h, a : a + 1],
                    accum_out=total[:, h, a : a + 1],
                )

        for half in range(2):
            turn_block(logits[:, 1], logits[:, 0], half)
            exponentials(0, half)
        for half in range(2):
            exponentials(1, half)

        def divide(h, parts):
            nc.vector.reciprocal(out=total[:, h, :], in_=total[:, h, :])
            for part in range(parts):
                tiles = slice(part * TILES // parts, (part + 1) * TILES // parts)
                nc.vector.tensor_tensor(
                    out=share_runs[:, h, tiles, :],
                    in0=powers[:, h, tiles, :],
                    in1=total[:, h, tiles].unsqueeze(2).to_broadcast([P, TILES // parts, TOK]),
                    op=ALU.mult,
                )

        def store(out, rows):
            nc.sync.dma_start(
                out=out.rearrange("b g k s p -> (b g k s) p").rearrange("(i q) p -> q i p", q=P),
                in_=rows.rearrange("q (i p) -> q i p", p=SLOTS),
            )

        divide(0, 1)
        store(out_1, shares[:, 0, :])
        divide(1, 2)
        disp = keep.tile([P, used], F32, align_bytes=64)
        for half in range(2):
            turn_block(disp, shares[:, 1], half)
        store(out_0, disp[:])
